import numpy as np
import ml_dtypes


def mxq(x, axis, fmt="e4m3"):
    dtype, down = {"e4m3": (ml_dtypes.float8_e4m3fn, 7), "e5m2": (ml_dtypes.float8_e5m2, 14)}[fmt]
    v = np.moveaxis(np.asarray(x, np.float32).astype(ml_dtypes.bfloat16).astype(np.float64), axis, -1)
    blocks = v.reshape(v.shape[:-1] + (-1, 32))
    amax = np.abs(blocks).max(-1, keepdims=True)
    byte = np.maximum(np.where(amax > 0, np.frexp(amax)[1] - 1 + 127, 0) - down, 1)
    scale = np.exp2(byte - 127.0)
    codes = (blocks / scale).astype(np.float32).astype(dtype).astype(np.float64)
    return np.moveaxis((codes * scale).reshape(v.shape), -1, axis)


WIDE = False


def mx_kscale(k):
    if not WIDE:
        return np.ones(k)
    levels = np.array([10, -10, 5, -5, 0])
    a = np.random.permutation(np.resize(levels, k // 512 * 4)).reshape(k // 512, 4)
    idx = np.arange(k)
    return np.exp2(a[idx // 512, idx % 128 // 32])


BF16 = ml_dtypes.bfloat16


def bf(x):
    return np.asarray(x, np.float32).astype(BF16)


def f64(x):
    return np.asarray(x).astype(np.float64)


B, Nb1, Nw1, Nb2x, Nb2y, Nw2x, Nw2y, R, C = 4096, 2, 16, 4, 4, 16, 16, 16, 2
J1 = Nb1 * Nb1
K1 = C * Nw1 * Nw1
J3 = Nb2x * Nb2y
L1 = J3 * R
J2 = J3 * J1


def setup_inputs():
    s = mx_kscale(K1)
    sx = s.reshape(Nw1, Nw1, C)[:, None, :, :]
    x = np.random.standard_normal((B, Nb1, Nw1, Nb1, Nw1, C)) * sx
    return {"x": bf(x.reshape(B, Nb1 * Nw1 * Nb1 * Nw1, C)),
            "k1": bf(np.random.standard_normal((J1, K1, L1)) / np.sqrt(K1) / s[None, :, None]),
            "b1": bf(np.random.standard_normal((1, J1, L1)) * 0.3)}


def reference(x, k1, b1):
    h = f64(x).reshape(B, Nb1, Nw1, Nb1, Nw1, C).transpose(0, 1, 3, 2, 4, 5).reshape(B, J1, K1)
    hq = mxq(h, 2, "e4m3").transpose(1, 0, 2)
    y = (hq @ mxq(f64(k1), 1, "e4m3")).transpose(1, 0, 2) + f64(b1)
    y = y.reshape(B, J1, J3, R).transpose(0, 3, 1, 2)
    return y.reshape(B, J2, R)

@@ -1,0 +1,187 @@
+from contextlib import ExitStack
+
+import concourse.mybir as mybir
+from concourse.masks import make_identity
+
+FLOPS = 2 * 4096 * 4 * 512 * 256
+
+F32 = mybir.dt.float32
+BF16 = mybir.dt.bfloat16
+U32 = mybir.dt.uint32
+U8 = mybir.dt.uint8
+FP8X4 = mybir.dt.float8_e4m3fn_x4
+ADD = mybir.AluOpType.add
+MULT = mybir.AluOpType.mult
+COPY = mybir.ActivationFunctionType.Copy
+
+P = 128
+SUB = 2
+NCH = 4096 // (P * SUB)
+PREFETCH = 5
+LAG = 1
+
+
+def tile_switchnet_fstar_pa_t_kernel(tc, x, k1, b1, out):
+    nc = tc.nc
+    x_v = x.rearrange("(n p t) g c -> n p (t g c)", p=P, t=SUB)
+    out_v = out.rearrange("(n p t) a b -> n p (t a b)", p=P, t=SUB)
+
+    with ExitStack() as ctx:
+        const = ctx.enter_context(tc.tile_pool(name="const", bufs=1))
+        xin = ctx.enter_context(tc.tile_pool(name="xin", bufs=PREFETCH + 1))
+        grp = ctx.enter_context(tc.tile_pool(name="grp", bufs=3))
+        cod = ctx.enter_context(tc.tile_pool(name="cod", bufs=3))
+        outs = ctx.enter_context(tc.tile_pool(name="outs", bufs=4))
+        psx = ctx.enter_context(tc.psum_pool(name="psx", bufs=4))
+        psa = ctx.enter_context(tc.psum_pool(name="psa", bufs=4))
+
+        x_tiles = {}
+
+        def load(n):
+            xs = xin.tile([P, SUB * 2048], BF16)
+            nc.scalar.dma_start(out=xs[:], in_=x_v[n])
+            x_tiles[n] = xs
+
+        wraw = const.tile([P, 2, 8, 256], BF16)
+        load(0)
+        for br in range(2):
+            for r in range(4):
+                for bc in range(2):
+                    p0 = r * 32 + bc * 16
+                    src = k1[br * 2 + bc].rearrange(
+                        "(u r c h) l -> r c u (h l)", u=4, r=4, c=16, h=2
+                    )[r]
+                    nc.sync.dma_start(
+                        out=wraw[p0 : p0 + 16, br].rearrange("p (u h) l -> p u (h l)", h=2), in_=src
+                    )
+            load(1 + br)
+        for n in range(3, PREFETCH):
+            load(n)
+
+        ident = const.tile([P, P], F32)
+        make_identity(nc, ident[:])
+        mask = const.tile([P, 2], F32)
+        nc.vector.tensor_reduce(
+            out=mask[:],
+            in_=ident[:].rearrange("p (g h c) -> p h g c", g=4, h=2, c=16),
+            axis=mybir.AxisListType.XY,
+            op=ADD,
+        )
+
+        brow = const.tile([P, 1024], BF16)
+        nc.vector.memset(brow[:], 0.0)
+        nc.sync.dma_start(out=brow[0:1, :], in_=b1.rearrange("o j l -> o (j l)"))
+        ones = const.tile([P, P], BF16)
+        nc.vector.memset(ones[:], 1.0)
+        bias = const.tile([P, 2, 16, 2, 16], F32)
+
+        wg = const.tile([P, 4 * 2048], BF16, align_bytes=64)
+        wc = const.tile([P, 4 * 512], U32, align_bytes=64)
+        wp = const.tile([P, 4 * 512], U8, align_bytes=64)
+        on_scalar = {(0, 1, 0), (1, 0, 0), (1, 1, 0)}
+        for br in range(2):
+            for s in range(2):
+                q = br * 2 + s
+                src = wraw[:, br, 4 * s : 4 * s + 4, :].rearrange(
+                    "p t (m r) -> p r m t", m=16, r=16
+                )
+                dst = wg[:, q * 2048 : (q + 1) * 2048].rearrange(
+                    "p (r c m t) -> p c r m t", r=16, c=2, m=16, t=4
+                )
+                for bcc in range(2):
+                    if (br, s, bcc) in on_scalar:
+                        nc.scalar.activation(
+                            out=dst[:, bcc], in_=src, func=COPY, scale=mask[:, bcc : bcc + 1]
+                        )
+                    else:
+                        nc.vector.tensor_scalar(
+                            out=dst[:, bcc],
+                            in0=src,
+                            scalar1=mask[:, bcc : bcc + 1],
+                            scalar2=None,
+                            op0=MULT,
+                        )
+                nc.vector.quantize_mx(
+                    out=wc[:, q * 512 : (q + 1) * 512].bitcast(FP8X4),
+                    scales=wp[:, q * 512 : (q + 1) * 512],
+                    in_=wg[:, q * 2048 : (q + 1) * 2048],
+                )
+
+        for br in range(2):
+            pb = psa.tile([P, 512], F32, tag="acc")
+            nc.tensor.matmul(
+                pb[:], lhsT=ones[:], rhs=brow[:, br * 512 : (br + 1) * 512], start=True, stop=True
+            )
+            nc.vector.tensor_copy(
+                out=bias[:, br], in_=pb[:].rearrange("p (c m r) -> p r c m", c=2, m=16, r=16)
+            )
+
+        codes = {}
+        planes = {}
+
+        def front(n):
+            xw = x_tiles[n][:].bitcast(F32)
+            g = grp.tile([P, SUB * 2048], BF16, align_bytes=64)
+            gf = g[:].bitcast(F32).rearrange(
+                "p (t r s b u) -> p t r s b u", t=SUB, r=2, s=2, b=P, u=2
+            )
+            banks = []
+            for t in range(SUB):
+                for br in range(2):
+                    ps = psx.tile([P, 4, P], F32, tag="xt")
+                    for u in range(4):
+                        c0 = t * 1024 + br * 512 + u * P
+                        nc.tensor.transpose(ps[:, u, :], xw[:, c0 : c0 + P], ident[:])
+                    banks.append((t, br, ps))
+            for t, br, ps in banks:
+                nc.scalar.copy(
+                    out=gf[:, t, br], in_=ps[:].rearrange("p (s u) b -> p s b u", u=2)
+                )
+            cw = cod.tile([P, SUB * 512], U32, align_bytes=64)
+            cp = cod.tile([P, SUB * 512], U8, align_bytes=64)
+            for t in range(SUB):
+                nc.vector.quantize_mx(
+                    out=cw[:, t * 512 : (t + 1) * 512].bitcast(FP8X4),
+                    scales=cp[:, t * 512 : (t + 1) * 512],
+                    in_=g[:, t * 2048 : (t + 1) * 2048],
+                )
+            codes[n] = cw
+            planes[n] = cp
+
+        def back(n):
+            cw = codes[n]
+            cp = planes[n]
+            ob = outs.tile([P, SUB, 16, 2, 32], F32)
+            accs = []
+            for t in range(SUB):
+                for br in range(2):
+                    acc = psa.tile([P, 512], F32, tag="acc")
+                    for s in range(2):
+                        c0 = ((t * 2 + br) * 2 + s) * P
+                        w0 = (br * 2 + s) * 512
+                        nc.tensor.matmul_mx(
+                            out=acc[:],
+                            lhsT=cw[:, c0 : c0 + P].bitcast(FP8X4),
+                            lhsT_scale=cp[:, c0 : c0 + P],
+                            rhs=wc[:, w0 : w0 + 512].bitcast(FP8X4),
+                            rhs_scale=wp[:, w0 : w0 + 512],
+                            start=(s == 0),
+                            stop=(s == 1),
+                        )
+                    accs.append((t, br, acc))
+            for t, br, acc in accs:
+                nc.vector.tensor_tensor(
+                    out=ob[:, t, :, br, :],
+                    in0=acc[:].rearrange("p (r q) -> p r q", q=32),
+                    in1=bias[:, br].rearrange("p r c m -> p r (c m)"),
+                    op=ADD,
+                )
+            nc.sync.dma_start(out=out_v[n], in_=ob[:].rearrange("p t r b q -> p (t r b q)"))
+
+        for n in range(NCH + LAG):
+            if n < NCH:
+                front(n)
+                if n + PREFETCH < NCH:
+                    load(n + PREFETCH)
+            if n >= LAG:
+                back(n - LAG)

@@ -17,142 +17,75 @@ COPY = mybir.ActivationFunctionType.Copy
 P = 128
 SUB = 2
 NCH = 4096 // (P * SUB)
-PREFETCH = 5
-LAG = 1
+XBUFS = 8
 
 
 def tile_switchnet_fstar_pa_t_kernel(tc, x, k1, b1, out):
     nc = tc.nc
     x_v = x.rearrange("(n p t) g c -> n p (t g c)", p=P, t=SUB)
-    out_v = out.rearrange("(n p t) a b -> n p (t a b)", p=P, t=SUB)
+    out_v = out.rearrange("(n p t) a b -> n p t (a b)", p=P, t=SUB)
 
     with ExitStack() as ctx:
         const = ctx.enter_context(tc.tile_pool(name="const", bufs=1))
-        xin = ctx.enter_context(tc.tile_pool(name="xin", bufs=PREFETCH + 1))
+        xin = ctx.enter_context(tc.tile_pool(name="xin", bufs=XBUFS))
         grp = ctx.enter_context(tc.tile_pool(name="grp", bufs=3))
         cod = ctx.enter_context(tc.tile_pool(name="cod", bufs=3))
         outs = ctx.enter_context(tc.tile_pool(name="outs", bufs=4))
         psx = ctx.enter_context(tc.psum_pool(name="psx", bufs=4))
         psa = ctx.enter_context(tc.psum_pool(name="psa", bufs=4))
+        ctx.enter_context(tc.manual_schedule())
 
         x_tiles = {}
+        banks = {}
+        groups = {}
+        codes = {}
+        planes = {}
+        accs = {}
+        obs = {}
 
         def load(n):
             xs = xin.tile([P, SUB * 2048], BF16)
-            nc.scalar.dma_start(out=xs[:], in_=x_v[n])
+            nc.gpsimd.dma_start(out=xs[:], in_=x_v[n])
             x_tiles[n] = xs
 
-        wraw = const.tile([P, 2, 8, 256], BF16)
-        load(0)
-        for br in range(2):
-            for r in range(4):
-                for bc in range(2):
-                    p0 = r * 32 + bc * 16
-                    src = k1[br * 2 + bc].rearrange(
-                        "(u r c h) l -> r c u (h l)", u=4, r=4, c=16, h=2
-                    )[r]
-                    nc.sync.dma_start(
-                        out=wraw[p0 : p0 + 16, br].rearrange("p (u h) l -> p u (h l)", h=2), in_=src
-                    )
-            load(1 + br)
-        for n in range(3, PREFETCH):
-            load(n)
-
-        ident = const.tile([P, P], F32)
-        make_identity(nc, ident[:])
-        mask = const.tile([P, 2], F32)
-        nc.vector.tensor_reduce(
-            out=mask[:],
-            in_=ident[:].rearrange("p (g h c) -> p h g c", g=4, h=2, c=16),
-            axis=mybir.AxisListType.XY,
-            op=ADD,
-        )
-
-        brow = const.tile([P, 1024], BF16)
-        nc.vector.memset(brow[:], 0.0)
-        nc.sync.dma_start(out=brow[0:1, :], in_=b1.rearrange("o j l -> o (j l)"))
-        ones = const.tile([P, P], BF16)
-        nc.vector.memset(ones[:], 1.0)
-        bias = const.tile([P, 2, 16, 2, 16], F32)
-
-        wg = const.tile([P, 4 * 2048], BF16, align_bytes=64)
-        wc = const.tile([P, 4 * 512], U32, align_bytes=64)
-        wp = const.tile([P, 4 * 512], U8, align_bytes=64)
-        on_scalar = {(0, 1, 0), (1, 0, 0), (1, 1, 0)}
-        for br in range(2):
-            for s in range(2):
-                q = br * 2 + s
-                src = wraw[:, br, 4 * s : 4 * s + 4, :].rearrange(
-                    "p t (m r) -> p r m t", m=16, r=16
-                )
-                dst = wg[:, q * 2048 : (q + 1) * 2048].rearrange(
-                    "p (r c m t) -> p c r m t", r=16, c=2, m=16, t=4
-                )
-                for bcc in range(2):
-                    if (br, s, bcc) in on_scalar:
-                        nc.scalar.activation(
-                            out=dst[:, bcc], in_=src, func=COPY, scale=mask[:, bcc : bcc + 1]
-                        )
-                    else:
-                        nc.vector.tensor_scalar(
-                            out=dst[:, bcc],
-                            in0=src,
-                            scalar1=mask[:, bcc : bcc + 1],
-                            scalar2=None,
-                            op0=MULT,
-                        )
-                nc.vector.quantize_mx(
-                    out=wc[:, q * 512 : (q + 1) * 512].bitcast(FP8X4),
-                    scales=wp[:, q * 512 : (q + 1) * 512],
-                    in_=wg[:, q * 2048 : (q + 1) * 2048],
-                )
-
-        for br in range(2):
-            pb = psa.tile([P, 512], F32, tag="acc")
-            nc.tensor.matmul(
-                pb[:], lhsT=ones[:], rhs=brow[:, br * 512 : (br + 1) * 512], start=True, stop=True
-            )
-            nc.vector.tensor_copy(
-                out=bias[:, br], in_=pb[:].rearrange("p (c m r) -> p r c m", c=2, m=16, r=16)
-            )
-
-        codes = {}
-        planes = {}
-
-        def front(n):
+        def transposes(n):
             xw = x_tiles[n][:].bitcast(F32)
-            g = grp.tile([P, SUB * 2048], BF16, align_bytes=64)
-            gf = g[:].bitcast(F32).rearrange(
-                "p (t r s b u) -> p t r s b u", t=SUB, r=2, s=2, b=P, u=2
-            )
-            banks = []
             for t in range(SUB):
                 for br in range(2):
                     ps = psx.tile([P, 4, P], F32, tag="xt")
                     for u in range(4):
                         c0 = t * 1024 + br * 512 + u * P
                         nc.tensor.transpose(ps[:, u, :], xw[:, c0 : c0 + P], ident[:])
-                    banks.append((t, br, ps))
-            for t, br, ps in banks:
-                nc.scalar.copy(
-                    out=gf[:, t, br], in_=ps[:].rearrange("p (s u) b -> p s b u", u=2)
-                )
-            cw = cod.tile([P, SUB * 512], U32, align_bytes=64)
-            cp = cod.tile([P, SUB * 512], U8, align_bytes=64)
-            for t in range(SUB):
-                nc.vector.quantize_mx(
-                    out=cw[:, t * 512 : (t + 1) * 512].bitcast(FP8X4),
-                    scales=cp[:, t * 512 : (t + 1) * 512],
-                    in_=g[:, t * 2048 : (t + 1) * 2048],
-                )
-            codes[n] = cw
-            planes[n] = cp
+                    banks[(n, t, br)] = ps
 
-        def back(n):
+        def copy_out(n, t):
+            if t == 0:
+                g = grp.tile([P, SUB * 2048], BF16, align_bytes=64)
+                groups[n] = g
+            gf = groups[n][:].bitcast(F32).rearrange(
+                "p (t r s b u) -> p t r s b u", t=SUB, r=2, s=2, b=P, u=2
+            )
+            for br in range(2):
+                nc.scalar.copy(
+                    out=gf[:, t, br],
+                    in_=banks[(n, t, br)][:].rearrange("p (s u) b -> p s b u", u=2),
+                )
+
+        def quantise(n, t):
+            if t == 0:
+                cw = cod.tile([P, SUB * 512], U32, align_bytes=64)
+                cp = cod.tile([P, SUB * 512], U8, align_bytes=64)
+                codes[n] = cw
+                planes[n] = cp
+            nc.vector.quantize_mx(
+                out=codes[n][:, t * 512 : (t + 1) * 512].bitcast(FP8X4),
+                scales=planes[n][:, t * 512 : (t + 1) * 512],
+                in_=groups[n][:, t * 2048 : (t + 1) * 2048],
+            )
+
+        def multiply(n):
             cw = codes[n]
             cp = planes[n]
-            ob = outs.tile([P, SUB, 16, 2, 32], F32)
-            accs = []
             for t in range(SUB):
                 for br in range(2):
                     acc = psa.tile([P, 512], F32, tag="acc")
@@ -168,20 +101,123 @@ def tile_switchnet_fstar_pa_t_kernel(tc, x, k1, b1, out):
                             start=(s == 0),
                             stop=(s == 1),
                         )
-                    accs.append((t, br, acc))
-            for t, br, acc in accs:
+                    accs[(n, t, br)] = acc
+
+        def add_bias(n, t):
+            if t == 0:
+                ob = outs.tile([P, SUB, 16, 2, 2, 16], F32)
+                obs[n] = ob
+            for br in range(2):
                 nc.vector.tensor_tensor(
-                    out=ob[:, t, :, br, :],
-                    in0=acc[:].rearrange("p (r q) -> p r q", q=32),
-                    in1=bias[:, br].rearrange("p r c m -> p r (c m)"),
+                    out=obs[n][:, t, :, br],
+                    in0=accs[(n, t, br)][:].rearrange("p (c m r) -> p r c m", c=2, m=16, r=16),
+                    in1=bias[:, br],
                     op=ADD,
                 )
-            nc.sync.dma_start(out=out_v[n], in_=ob[:].rearrange("p t r b q -> p (t r b q)"))
 
-        for n in range(NCH + LAG):
-            if n < NCH:
-                front(n)
-                if n + PREFETCH < NCH:
-                    load(n + PREFETCH)
-            if n >= LAG:
-                back(n - LAG)
+        load(0)
+        ident = const.tile([P, P], F32)
+        make_identity(nc, ident[:])
+        for n in range(1, XBUFS):
+            load(n)
+
+        wraw = const.tile([P, 2, 8, 256], BF16)
+        for br in range(2):
+            for r in range(4):
+                for bc in range(2):
+                    p0 = r * 32 + bc * 16
+                    src = k1[br * 2 + bc].rearrange(
+                        "(u r c h) l -> r c u (h l)", u=4, r=4, c=16, h=2
+                    )[r]
+                    nc.sync.dma_start(
+                        out=wraw[p0 : p0 + 16, br].rearrange("p (u h) l -> p u (h l)", h=2), in_=src
+                    )
+        brow = const.tile([P, 1024], BF16)
+        nc.vector.memset(brow[:], 0.0)
+        nc.sync.dma_start(out=brow[0:1, :], in_=b1.rearrange("o j l -> o (j l)"))
+        ones = const.tile([P, P], BF16)
+        nc.vector.memset(ones[:], 1.0)
+        mask = const.tile([P, 2], F32)
+        nc.vector.tensor_reduce(
+            out=mask[:],
+            in_=ident[:].rearrange("p (g h c) -> p h g c", g=4, h=2, c=16),
+            axis=mybir.AxisListType.XY,
+            op=ADD,
+        )
+        bias = const.tile([P, 2, 16, 2, 16], F32)
+
+        wg = const.tile([P, 4 * 2048], BF16, align_bytes=64)
+        wc = const.tile([P, 4 * 512], U32, align_bytes=64)
+        wp = const.tile([P, 4 * 512], U8, align_bytes=64)
+
+        def w_piece(br, s, bcc, on_scalar):
+            o0 = (br * 2 + s) * 2048 + bcc * 1024
+            src = wraw[:, br, 4 * s : 4 * s + 4, :].rearrange("p t (c i) -> p c t i", i=4)
+            dst = wg[:, o0 : o0 + 1024].rearrange("p (c i t) -> p c t i", i=4, t=4)
+            if on_scalar:
+                nc.scalar.activation(out=dst, in_=src, func=COPY, scale=mask[:, bcc : bcc + 1])
+            else:
+                nc.vector.tensor_scalar(
+                    out=dst, in0=src, scalar1=mask[:, bcc : bcc + 1], scalar2=None, op0=MULT
+                )
+
+        def w_quantise(br, s):
+            q = br * 2 + s
+            nc.vector.quantize_mx(
+                out=wc[:, q * 512 : (q + 1) * 512].bitcast(FP8X4),
+                scales=wp[:, q * 512 : (q + 1) * 512],
+                in_=wg[:, q * 2048 : (q + 1) * 2048],
+            )
+
+        w_piece(0, 1, 1, True)
+        w_piece(0, 0, 0, False)
+        w_piece(0, 0, 1, False)
+        w_piece(0, 1, 0, False)
+        w_quantise(0, 0)
+        w_quantise(0, 1)
+        transposes(0)
+        copy_out(0, 0)
+        w_piece(1, 1, 1, True)
+        copy_out(0, 1)
+        w_piece(1, 0, 0, False)
+        w_piece(1, 0, 1, False)
+        w_piece(1, 1, 0, False)
+        quantise(0, 0)
+        w_quantise(1, 0)
+        w_quantise(1, 1)
+        quantise(0, 1)
+        for br in range(2):
+            pb = psa.tile([P, 512], F32, tag="acc")
+            nc.tensor.matmul(
+                pb[:], lhsT=ones[:], rhs=brow[:, br * 512 : (br + 1) * 512], start=True, stop=True
+            )
+            nc.scalar.copy(
+                out=bias[:, br], in_=pb[:].rearrange("p (c m r) -> p r c m", c=2, m=16, r=16)
+            )
+
+        for n in range(NCH):
+            more = n + 1 < NCH
+            if more:
+                transposes(n + 1)
+                copy_out(n + 1, 0)
+                copy_out(n + 1, 1)
+            if n + XBUFS < NCH:
+                load(n + XBUFS)
+            multiply(n)
+            add_bias(n, 0)
+            if not more:
+                nc.sync.dma_start(
+                    out=out_v[n][:, 0, :], in_=obs[n][:, 0].rearrange("p r b c m -> p (r b c m)")
+                )
+            if more:
+                quantise(n + 1, 0)
+            add_bias(n, 1)
+            if more:
+                quantise(n + 1, 1)
+                nc.sync.dma_start(
+                    out=out_v[n], in_=obs[n][:].rearrange("p t r b c m -> p t (r b c m)")
+                )
+            else:
+                nc.sync.dma_start(
+                    out=out_v[n][:, 1, :], in_=obs[n][:, 1].rearrange("p r b c m -> p (r b c m)")
+                )

@@ -22,7 +22,7 @@ XBUFS = 8
 
 def tile_switchnet_fstar_pa_t_kernel(tc, x, k1, b1, out):
     nc = tc.nc
-    x_v = x.rearrange("(n p t) g c -> n p (t g c)", p=P, t=SUB)
+    x_v = x.rearrange("(n p t) g c -> n p t (g c)", p=P, t=SUB)
     out_v = out.rearrange("(n p t) a b -> n p t (a b)", p=P, t=SUB)
 
     with ExitStack() as ctx:
@@ -45,7 +45,11 @@ def tile_switchnet_fstar_pa_t_kernel(tc, x, k1, b1, out):
 
         def load(n):
             xs = xin.tile([P, SUB * 2048], BF16)
-            nc.gpsimd.dma_start(out=xs[:], in_=x_v[n])
+            if n == 0:
+                for t in range(SUB):
+                    nc.gpsimd.dma_start(out=xs[:, t * 2048 : (t + 1) * 2048], in_=x_v[n][:, t, :])
+            else:
+                nc.gpsimd.dma_start(out=xs[:].rearrange("p (t e) -> p t e", t=SUB), in_=x_v[n])
             x_tiles[n] = xs
 
         def transposes(n):
@@ -83,11 +87,16 @@ def tile_switchnet_fstar_pa_t_kernel(tc, x, k1, b1, out):
                 in_=groups[n][:, t * 2048 : (t + 1) * 2048],
             )
 
+        def bank_order(n):
+            if n == 0:
+                return [(0, 0), (1, 0), (0, 1), (1, 1)]
+            return [(0, 0), (0, 1), (1, 0), (1, 1)]
+
         def multiply(n):
             cw = codes[n]
             cp = planes[n]
-            for t in range(SUB):
-                for br in range(2):
+            for t, br in bank_order(n):
+                for once in range(1):
                     acc = psa.tile([P, 512], F32, tag="acc")
                     for s in range(2):
                         c0 = ((t * 2 + br) * 2 + s) * P
@@ -103,11 +112,11 @@ def tile_switchnet_fstar_pa_t_kernel(tc, x, k1, b1, out):
                         )
                     accs[(n, t, br)] = acc
 
-        def add_bias(n, t):
-            if t == 0:
+        def add_bias(n, half):
+            if half == 0:
                 ob = outs.tile([P, SUB, 16, 2, 2, 16], F32)
                 obs[n] = ob
-            for br in range(2):
+            for t, br in bank_order(n)[2 * half : 2 * half + 2]:
                 nc.vector.tensor_tensor(
                     out=obs[n][:, t, :, br],
                     in0=accs[(n, t, br)][:].rearrange("p (c m r) -> p r c m", c=2, m=16, r=16),
@@ -115,21 +124,21 @@ def tile_switchnet_fstar_pa_t_kernel(tc, x, k1, b1, out):
                     op=ADD,
                 )
 
-        load(0)
         ident = const.tile([P, P], F32)
         make_identity(nc, ident[:])
-        for n in range(1, XBUFS):
+        for n in range(XBUFS):
             load(n)
 
         wraw = const.tile([P, 2, 8, 256], BF16)
         for br in range(2):
-            for r in range(4):
+            for r in (0, 2, 1, 3):
                 for bc in range(2):
                     p0 = r * 32 + bc * 16
                     src = k1[br * 2 + bc].rearrange(
                         "(u r c h) l -> r c u (h l)", u=4, r=4, c=16, h=2
                     )[r]
-                    nc.sync.dma_start(
+                    queue = nc.sync if bc == 0 else nc.scalar
+                    queue.dma_start(
                         out=wraw[p0 : p0 + 16, br].rearrange("p (u h) l -> p u (h l)", h=2), in_=src
                     )
         brow = const.tile([P, 1024], BF16)
@@ -177,15 +186,15 @@ def tile_switchnet_fstar_pa_t_kernel(tc, x, k1, b1, out):
         w_quantise(0, 1)
         transposes(0)
         copy_out(0, 0)
-        w_piece(1, 1, 1, True)
         copy_out(0, 1)
+        w_piece(1, 1, 1, True)
+        quantise(0, 0)
         w_piece(1, 0, 0, False)
         w_piece(1, 0, 1, False)
+        quantise(0, 1)
         w_piece(1, 1, 0, False)
-        quantise(0, 0)
         w_quantise(1, 0)
         w_quantise(1, 1)
-        quantise(0, 1)
         for br in range(2):
             pb = psa.tile([P, 512], F32, tag="acc")
             nc.tensor.matmul(

@@ -17,7 +17,9 @@ COPY = mybir.ActivationFunctionType.Copy
 P = 128
 SUB = 2
 NCH = 4096 // (P * SUB)
+NSUB = NCH * SUB
 XBUFS = 8
+LAG = 2
 
 
 def tile_switchnet_fstar_pa_t_kernel(tc, x, k1, b1, out):
@@ -28,8 +30,8 @@ def tile_switchnet_fstar_pa_t_kernel(tc, x, k1, b1, out):
     with ExitStack() as ctx:
         const = ctx.enter_context(tc.tile_pool(name="const", bufs=1))
         xin = ctx.enter_context(tc.tile_pool(name="xin", bufs=XBUFS))
-        grp = ctx.enter_context(tc.tile_pool(name="grp", bufs=3))
-        cod = ctx.enter_context(tc.tile_pool(name="cod", bufs=3))
+        grp = ctx.enter_context(tc.tile_pool(name="grp", bufs=4))
+        cod = ctx.enter_context(tc.tile_pool(name="cod", bufs=LAG + 3))
         outs = ctx.enter_context(tc.tile_pool(name="outs", bufs=4))
         psx = ctx.enter_context(tc.psum_pool(name="psx", bufs=4))
         psa = ctx.enter_context(tc.psum_pool(name="psa", bufs=4))
@@ -52,77 +54,54 @@ def tile_switchnet_fstar_pa_t_kernel(tc, x, k1, b1, out):
                 nc.gpsimd.dma_start(out=xs[:].rearrange("p (t e) -> p t e", t=SUB), in_=x_v[n])
             x_tiles[n] = xs
 
-        def transposes(n):
-            xw = x_tiles[n][:].bitcast(F32)
-            for t in range(SUB):
-                for br in range(2):
-                    ps = psx.tile([P, 4, P], F32, tag="xt")
-                    for u in range(4):
-                        c0 = t * 1024 + br * 512 + u * P
-                        nc.tensor.transpose(ps[:, u, :], xw[:, c0 : c0 + P], ident[:])
-                    banks[(n, t, br)] = ps
+        def transposes(i):
+            xw = x_tiles[i // SUB][:].bitcast(F32)
+            for br in range(2):
+                ps = psx.tile([P, 4, P], F32, tag="xt")
+                for u in range(4):
+                    c0 = (i % SUB) * 1024 + br * 512 + u * P
+                    nc.tensor.transpose(ps[:, u, :], xw[:, c0 : c0 + P], ident[:])
+                banks[(i, br)] = ps
 
-        def copy_out(n, t):
-            if t == 0:
-                g = grp.tile([P, SUB * 2048], BF16, align_bytes=64)
-                groups[n] = g
-            gf = groups[n][:].bitcast(F32).rearrange(
-                "p (t r s b u) -> p t r s b u", t=SUB, r=2, s=2, b=P, u=2
-            )
+        def copy_out(i):
+            g = grp.tile([P, 2048], BF16, align_bytes=64)
+            groups[i] = g
+            gf = g[:].bitcast(F32).rearrange("p (r s b u) -> p r s b u", r=2, s=2, b=P, u=2)
             for br in range(2):
                 nc.scalar.copy(
-                    out=gf[:, t, br],
-                    in_=banks[(n, t, br)][:].rearrange("p (s u) b -> p s b u", u=2),
+                    out=gf[:, br], in_=banks[(i, br)][:].rearrange("p (s u) b -> p s b u", u=2)
                 )
 
-        def quantise(n, t):
-            if t == 0:
-                cw = cod.tile([P, SUB * 512], U32, align_bytes=64)
-                cp = cod.tile([P, SUB * 512], U8, align_bytes=64)
-                codes[n] = cw
-                planes[n] = cp
-            nc.vector.quantize_mx(
-                out=codes[n][:, t * 512 : (t + 1) * 512].bitcast(FP8X4),
-                scales=planes[n][:, t * 512 : (t + 1) * 512],
-                in_=groups[n][:, t * 2048 : (t + 1) * 2048],
+        def quantise(i):
+            cw = cod.tile([P, 512], U32, align_bytes=64)
+            cp = cod.tile([P, 512], U8, align_bytes=64)
+            codes[i] = cw
+            planes[i] = cp
+            nc.vector.quantize_mx(out=cw[:].bitcast(FP8X4), scales=cp[:], in_=groups[i][:])
+
+        def multiply(i, br):
+            acc = psa.tile([P, 512], F32, tag="acc")
+            for s in range(2):
+                c0 = (br * 2 + s) * P
+                w0 = (br * 2 + s) * 512
+                nc.tensor.matmul_mx(
+                    out=acc[:],
+                    lhsT=codes[i][:, c0 : c0 + P].bitcast(FP8X4),
+                    lhsT_scale=planes[i][:, c0 : c0 + P],
+                    rhs=wc[:, w0 : w0 + 512].bitcast(FP8X4),
+                    rhs_scale=wp[:, w0 : w0 + 512],
+                    start=(s == 0),
+                    stop=(s == 1),
+                )
+            accs[(i, br)] = acc
+
+        def add_bias(i, br):
+            nc.vector.tensor_tensor(
+                out=obs[i // SUB][:, i % SUB, :, br],
+                in0=accs[(i, br)][:].rearrange("p (c m r) -> p r c m", c=2, m=16, r=16),
+                in1=bias[:, br],
+                op=ADD,
             )
-
-        def bank_order(n):
-            if n == 0:
-                return [(0, 0), (1, 0), (0, 1), (1, 1)]
-            return [(0, 0), (0, 1), (1, 0), (1, 1)]
-
-        def multiply(n):
-            cw = codes[n]
-            cp = planes[n]
-            for t, br in bank_order(n):
-                for once in range(1):
-                    acc = psa.tile([P, 512], F32, tag="acc")
-                    for s in range(2):
-                        c0 = ((t * 2 + br) * 2 + s) * P
-                        w0 = (br * 2 + s) * 512
-                        nc.tensor.matmul_mx(
-                            out=acc[:],
-                            lhsT=cw[:, c0 : c0 + P].bitcast(FP8X4),
-                            lhsT_scale=cp[:, c0 : c0 + P],
-                            rhs=wc[:, w0 : w0 + 512].bitcast(FP8X4),
-                            rhs_scale=wp[:, w0 : w0 + 512],
-                            start=(s == 0),
-                            stop=(s == 1),
-                        )
-                    accs[(n, t, br)] = acc
-
-        def add_bias(n, half):
-            if half == 0:
-                ob = outs.tile([P, SUB, 16, 2, 2, 16], F32)
-                obs[n] = ob
-            for t, br in bank_order(n)[2 * half : 2 * half + 2]:
-                nc.vector.tensor_tensor(
-                    out=obs[n][:, t, :, br],
-                    in0=accs[(n, t, br)][:].rearrange("p (c m r) -> p r c m", c=2, m=16, r=16),
-                    in1=bias[:, br],
-                    op=ADD,
-                )
 
         ident = const.tile([P, P], F32)
         make_identity(nc, ident[:])
@@ -185,13 +164,15 @@ def tile_switchnet_fstar_pa_t_kernel(tc, x, k1, b1, out):
         w_quantise(0, 0)
         w_quantise(0, 1)
         transposes(0)
-        copy_out(0, 0)
-        copy_out(0, 1)
+        copy_out(0)
+        transposes(1)
+        copy_out(1)
+        load(XBUFS)
         w_piece(1, 1, 1, True)
-        quantise(0, 0)
+        quantise(0)
         w_piece(1, 0, 0, False)
         w_piece(1, 0, 1, False)
-        quantise(0, 1)
+        quantise(1)
         w_piece(1, 1, 0, False)
         w_quantise(1, 0)
         w_quantise(1, 1)
@@ -204,29 +185,34 @@ def tile_switchnet_fstar_pa_t_kernel(tc, x, k1, b1, out):
                 out=bias[:, br], in_=pb[:].rearrange("p (c m r) -> p r c m", c=2, m=16, r=16)
             )
 
-        for n in range(NCH):
-            more = n + 1 < NCH
-            if more:
-                transposes(n + 1)
-                copy_out(n + 1, 0)
-                copy_out(n + 1, 1)
-            if n + XBUFS < NCH:
-                load(n + XBUFS)
-            multiply(n)
-            add_bias(n, 0)
-            if not more:
+        for i in range(NSUB):
+            n = i // SUB
+            if i + LAG < NSUB:
+                transposes(i + LAG)
+                copy_out(i + LAG)
+                if (i + LAG) % SUB == SUB - 1 and (i + LAG) // SUB + XBUFS < NCH:
+                    load((i + LAG) // SUB + XBUFS)
+            if i == 0:
+                pairs = [(0, 0), (1, 0)]
+            elif i == 1:
+                pairs = [(0, 1), (1, 1)]
+            else:
+                pairs = [(i, 0), (i, 1)]
+            if i % SUB == 0:
+                ob = outs.tile([P, SUB, 16, 2, 2, 16], F32)
+                obs[n] = ob
+            for j, br in pairs:
+                multiply(j, br)
+            for j, br in pairs:
+                add_bias(j, br)
+            if i + LAG < NSUB:
+                quantise(i + LAG)
+            if n == NCH - 1:
                 nc.sync.dma_start(
-                    out=out_v[n][:, 0, :], in_=obs[n][:, 0].rearrange("p r b c m -> p (r b c m)")
+                    out=out_v[n][:, i % SUB, :],
+                    in_=obs[n][:, i % SUB].rearrange("p r b c m -> p (r b c m)"),
                 )
-            if more:
-                quantise(n + 1, 0)
-            add_bias(n, 1)
-            if more:
-                quantise(n + 1, 1)
+            elif i % SUB == SUB - 1:
                 nc.sync.dma_start(
                     out=out_v[n], in_=obs[n][:].rearrange("p t r b c m -> p t (r b c m)")
-                )
-            else:
-                nc.sync.dma_start(
-                    out=out_v[n][:, 1, :], in_=obs[n][:, 1].rearrange("p r b c m -> p (r b c m)")
                 )

@@ -19,7 +19,9 @@ SUB = 2
 NCH = 4096 // (P * SUB)
 NSUB = NCH * SUB
 XBUFS = 8
-LAG = 2
+NBANK = NSUB * 2
+RUN = 3
+LEAD = 4
 
 
 def tile_switchnet_fstar_pa_t_kernel(tc, x, k1, b1, out):
@@ -30,8 +32,8 @@ def tile_switchnet_fstar_pa_t_kernel(tc, x, k1, b1, out):
     with ExitStack() as ctx:
         const = ctx.enter_context(tc.tile_pool(name="const", bufs=1))
         xin = ctx.enter_context(tc.tile_pool(name="xin", bufs=XBUFS))
-        grp = ctx.enter_context(tc.tile_pool(name="grp", bufs=4))
-        cod = ctx.enter_context(tc.tile_pool(name="cod", bufs=LAG + 3))
+        grp = ctx.enter_context(tc.tile_pool(name="grp", bufs=6))
+        cod = ctx.enter_context(tc.tile_pool(name="cod", bufs=LEAD + 2 * RUN))
         outs = ctx.enter_context(tc.tile_pool(name="outs", bufs=4))
         psx = ctx.enter_context(tc.psum_pool(name="psx", bufs=4))
         psa = ctx.enter_context(tc.psum_pool(name="psa", bufs=4))
@@ -44,6 +46,7 @@ def tile_switchnet_fstar_pa_t_kernel(tc, x, k1, b1, out):
         planes = {}
         accs = {}
         obs = {}
+        left = {}
 
         def load(n):
             xs = xin.tile([P, SUB * 2048], BF16)
@@ -54,54 +57,72 @@ def tile_switchnet_fstar_pa_t_kernel(tc, x, k1, b1, out):
                 nc.gpsimd.dma_start(out=xs[:].rearrange("p (t e) -> p t e", t=SUB), in_=x_v[n])
             x_tiles[n] = xs
 
-        def transposes(i):
+        def transposes(k):
+            i, br = k // 2, k % 2
             xw = x_tiles[i // SUB][:].bitcast(F32)
-            for br in range(2):
-                ps = psx.tile([P, 4, P], F32, tag="xt")
-                for u in range(4):
-                    c0 = (i % SUB) * 1024 + br * 512 + u * P
-                    nc.tensor.transpose(ps[:, u, :], xw[:, c0 : c0 + P], ident[:])
-                banks[(i, br)] = ps
+            ps = psx.tile([P, 4, P], F32, tag="xt")
+            for u in range(4):
+                c0 = (i % SUB) * 1024 + br * 512 + u * P
+                nc.tensor.transpose(ps[:, u, :], xw[:, c0 : c0 + P], ident[:])
+            banks[k] = ps
+            if k % (2 * SUB) == 2 * SUB - 1 and k // (2 * SUB) + XBUFS < NCH:
+                load(k // (2 * SUB) + XBUFS)
 
-        def copy_out(i):
-            g = grp.tile([P, 2048], BF16, align_bytes=64)
-            groups[i] = g
-            gf = g[:].bitcast(F32).rearrange("p (r s b u) -> p r s b u", r=2, s=2, b=P, u=2)
-            for br in range(2):
-                nc.scalar.copy(
-                    out=gf[:, br], in_=banks[(i, br)][:].rearrange("p (s u) b -> p s b u", u=2)
-                )
+        def copy_out(k):
+            g = grp.tile([P, 1024], BF16, align_bytes=64)
+            groups[k] = g
+            nc.scalar.copy(
+                out=g[:].bitcast(F32).rearrange("p (s b u) -> p s b u", s=2, b=P, u=2),
+                in_=banks[k][:].rearrange("p (s u) b -> p s b u", u=2),
+            )
 
-        def quantise(i):
-            cw = cod.tile([P, 512], U32, align_bytes=64)
-            cp = cod.tile([P, 512], U8, align_bytes=64)
-            codes[i] = cw
-            planes[i] = cp
-            nc.vector.quantize_mx(out=cw[:].bitcast(FP8X4), scales=cp[:], in_=groups[i][:])
+        def quantise(k):
+            cw = cod.tile([P, 256], U32, align_bytes=64)
+            cp = cod.tile([P, 256], U8, align_bytes=64)
+            codes[k] = cw
+            planes[k] = cp
+            nc.vector.quantize_mx(out=cw[:].bitcast(FP8X4), scales=cp[:], in_=groups[k][:])
 
-        def multiply(i, br):
+        def multiply(k):
+            br = k % 2
             acc = psa.tile([P, 512], F32, tag="acc")
             for s in range(2):
-                c0 = (br * 2 + s) * P
                 w0 = (br * 2 + s) * 512
                 nc.tensor.matmul_mx(
                     out=acc[:],
-                    lhsT=codes[i][:, c0 : c0 + P].bitcast(FP8X4),
-                    lhsT_scale=planes[i][:, c0 : c0 + P],
+                    lhsT=codes[k][:, s * P : (s + 1) * P].bitcast(FP8X4),
+                    lhsT_scale=planes[k][:, s * P : (s + 1) * P],
                     rhs=wc[:, w0 : w0 + 512].bitcast(FP8X4),
                     rhs_scale=wp[:, w0 : w0 + 512],
                     start=(s == 0),
                     stop=(s == 1),
                 )
-            accs[(i, br)] = acc
+            accs[k] = acc
 
-        def add_bias(i, br):
+        def add_bias(k):
+            i, br = k // 2, k % 2
+            n = i // SUB
+            if n not in obs:
+                ob = outs.tile([P, SUB, 16, 2, 2, 16], F32)
+                obs[n] = ob
+                left[n] = 2 * SUB
             nc.vector.tensor_tensor(
-                out=obs[i // SUB][:, i % SUB, :, br],
-                in0=accs[(i, br)][:].rearrange("p (c m r) -> p r c m", c=2, m=16, r=16),
+                out=obs[n][:, i % SUB, :, br],
+                in0=accs[k][:].rearrange("p (c m r) -> p r c m", c=2, m=16, r=16),
                 in1=bias[:, br],
                 op=ADD,
             )
+            left[n] = left[n] - 1
+            if n == NCH - 1:
+                if br == 1:
+                    nc.sync.dma_start(
+                        out=out_v[n][:, i % SUB, :],
+                        in_=obs[n][:, i % SUB].rearrange("p r b c m -> p (r b c m)"),
+                    )
+            elif left[n] == 0:
+                nc.sync.dma_start(
+                    out=out_v[n], in_=obs[n][:].rearrange("p t r b c m -> p t (r b c m)")
+                )
 
         ident = const.tile([P, P], F32)
         make_identity(nc, ident[:])
@@ -163,16 +184,16 @@ def tile_switchnet_fstar_pa_t_kernel(tc, x, k1, b1, out):
         w_piece(0, 1, 0, False)
         w_quantise(0, 0)
         w_quantise(0, 1)
-        transposes(0)
-        copy_out(0)
-        transposes(1)
-        copy_out(1)
-        load(XBUFS)
+        for k in range(LEAD):
+            transposes(k)
+            copy_out(k)
         w_piece(1, 1, 1, True)
         quantise(0)
+        quantise(1)
         w_piece(1, 0, 0, False)
         w_piece(1, 0, 1, False)
-        quantise(1)
+        quantise(2)
+        quantise(3)
         w_piece(1, 1, 0, False)
         w_quantise(1, 0)
         w_quantise(1, 1)
@@ -185,34 +206,17 @@ def tile_switchnet_fstar_pa_t_kernel(tc, x, k1, b1, out):
                 out=bias[:, br], in_=pb[:].rearrange("p (c m r) -> p r c m", c=2, m=16, r=16)
             )
 
-        for i in range(NSUB):
-            n = i // SUB
-            if i + LAG < NSUB:
-                transposes(i + LAG)
-                copy_out(i + LAG)
-                if (i + LAG) % SUB == SUB - 1 and (i + LAG) // SUB + XBUFS < NCH:
-                    load((i + LAG) // SUB + XBUFS)
-            if i == 0:
-                pairs = [(0, 0), (1, 0)]
-            elif i == 1:
-                pairs = [(0, 1), (1, 1)]
-            else:
-                pairs = [(i, 0), (i, 1)]
-            if i % SUB == 0:
-                ob = outs.tile([P, SUB, 16, 2, 2, 16], F32)
-                obs[n] = ob
-            for j, br in pairs:
-                multiply(j, br)
-            for j, br in pairs:
-                add_bias(j, br)
-            if i + LAG < NSUB:
-                quantise(i + LAG)
-            if n == NCH - 1:
-                nc.sync.dma_start(
-                    out=out_v[n][:, i % SUB, :],
-                    in_=obs[n][:, i % SUB].rearrange("p r b c m -> p (r b c m)"),
-                )
-            elif i % SUB == SUB - 1:
-                nc.sync.dma_start(
-                    out=out_v[n], in_=obs[n][:].rearrange("p t r b c m -> p t (r b c m)")
-                )
+        order = [0, 2, 1, 3] + list(range(4, NBANK))
+        for k0 in range(0, NBANK, RUN):
+            ahead = list(range(LEAD + k0, min(LEAD + k0 + RUN, NBANK)))
+            now = order[k0 : k0 + RUN]
+            for k in ahead:
+                transposes(k)
+                copy_out(k)
+            for k in now:
+                multiply(k)
+            for j in range(RUN):
+                if j < len(now):
+                    add_bias(now[j])
+                if j < len(ahead):
+                    quantise(ahead[j])

@@ -19,9 +19,7 @@ SUB = 2
 NCH = 4096 // (P * SUB)
 NSUB = NCH * SUB
 XBUFS = 8
-NBANK = NSUB * 2
-RUN = 3
-LEAD = 4
+LAG = 2
 
 
 def tile_switchnet_fstar_pa_t_kernel(tc, x, k1, b1, out):
@@ -32,8 +30,8 @@ def tile_switchnet_fstar_pa_t_kernel(tc, x, k1, b1, out):
     with ExitStack() as ctx:
         const = ctx.enter_context(tc.tile_pool(name="const", bufs=1))
         xin = ctx.enter_context(tc.tile_pool(name="xin", bufs=XBUFS))
-        grp = ctx.enter_context(tc.tile_pool(name="grp", bufs=6))
-        cod = ctx.enter_context(tc.tile_pool(name="cod", bufs=LEAD + 2 * RUN))
+        grp = ctx.enter_context(tc.tile_pool(name="grp", bufs=4))
+        cod = ctx.enter_context(tc.tile_pool(name="cod", bufs=LAG + 3))
         outs = ctx.enter_context(tc.tile_pool(name="outs", bufs=4))
         psx = ctx.enter_context(tc.psum_pool(name="psx", bufs=4))
         psa = ctx.enter_context(tc.psum_pool(name="psa", bufs=4))
@@ -46,7 +44,6 @@ def tile_switchnet_fstar_pa_t_kernel(tc, x, k1, b1, out):
         planes = {}
         accs = {}
         obs = {}
-        left = {}
 
         def load(n):
             xs = xin.tile([P, SUB * 2048], BF16)
@@ -57,72 +54,61 @@ def tile_switchnet_fstar_pa_t_kernel(tc, x, k1, b1, out):
                 nc.gpsimd.dma_start(out=xs[:].rearrange("p (t e) -> p t e", t=SUB), in_=x_v[n])
             x_tiles[n] = xs
 
-        def transposes(k):
-            i, br = k // 2, k % 2
+        def transposes(i):
             xw = x_tiles[i // SUB][:].bitcast(F32)
-            ps = psx.tile([P, 4, P], F32, tag="xt")
-            for u in range(4):
-                c0 = (i % SUB) * 1024 + br * 512 + u * P
-                nc.tensor.transpose(ps[:, u, :], xw[:, c0 : c0 + P], ident[:])
-            banks[k] = ps
-            if k % (2 * SUB) == 2 * SUB - 1 and k // (2 * SUB) + XBUFS < NCH:
-                load(k // (2 * SUB) + XBUFS)
+            for br in range(2):
+                ps = psx.tile([P, 4, P], F32, tag="xt")
+                for u in range(4):
+                    c0 = (i % SUB) * 1024 + br * 512 + u * P
+                    nc.tensor.transpose(ps[:, u, :], xw[:, c0 : c0 + P], ident[:])
+                banks[(i, br)] = ps
 
-        def copy_out(k):
-            g = grp.tile([P, 1024], BF16, align_bytes=64)
-            groups[k] = g
-            nc.scalar.copy(
-                out=g[:].bitcast(F32).rearrange("p (s b u) -> p s b u", s=2, b=P, u=2),
-                in_=banks[k][:].rearrange("p (s u) b -> p s b u", u=2),
-            )
+        def copy_out(i):
+            g = grp.tile([P, 2048], BF16, align_bytes=64)
+            groups[i] = g
+            gf = g[:].bitcast(F32).rearrange("p (r s b u) -> p r s b u", r=2, s=2, b=P, u=2)
+            for br in range(2):
+                nc.scalar.copy(
+                    out=gf[:, br], in_=banks[(i, br)][:].rearrange("p (s u) b -> p s b u", u=2)
+                )
 
-        def quantise(k):
-            cw = cod.tile([P, 256], U32, align_bytes=64)
-            cp = cod.tile([P, 256], U8, align_bytes=64)
-            codes[k] = cw
-            planes[k] = cp
-            nc.vector.quantize_mx(out=cw[:].bitcast(FP8X4), scales=cp[:], in_=groups[k][:])
+        def quantise(i):
+            cw = cod.tile([P, 512], U32, align_bytes=64)
+            cp = cod.tile([P, 512], U8, align_bytes=64)
+            codes[i] = cw
+            planes[i] = cp
+            nc.vector.quantize_mx(out=cw[:].bitcast(FP8X4), scales=cp[:], in_=groups[i][:])
 
-        def multiply(k):
-            br = k % 2
+        def multiply(i, br):
             acc = psa.tile([P, 512], F32, tag="acc")
             for s in range(2):
+                c0 = (br * 2 + s) * P
                 w0 = (br * 2 + s) * 512
                 nc.tensor.matmul_mx(
                     out=acc[:],
-                    lhsT=codes[k][:, s * P : (s + 1) * P].bitcast(FP8X4),
-                    lhsT_scale=planes[k][:, s * P : (s + 1) * P],
+                    lhsT=codes[i][:, c0 : c0 + P].bitcast(FP8X4),
+                    lhsT_scale=planes[i][:, c0 : c0 + P],
                     rhs=wc[:, w0 : w0 + 512].bitcast(FP8X4),
                     rhs_scale=wp[:, w0 : w0 + 512],
                     start=(s == 0),
                     stop=(s == 1),
                 )
-            accs[k] = acc
+            accs[(i, br)] = acc
 
-        def add_bias(k):
-            i, br = k // 2, k % 2
-            n = i // SUB
-            if n not in obs:
-                ob = outs.tile([P, SUB, 16, 2, 2, 16], F32)
-                obs[n] = ob
-                left[n] = 2 * SUB
+        def add_bias(i, br):
             nc.vector.tensor_tensor(
-                out=obs[n][:, i % SUB, :, br],
-                in0=accs[k][:].rearrange("p (c m r) -> p r c m", c=2, m=16, r=16),
+                out=obs[i // SUB][:, i % SUB, :, br],
+                in0=accs[(i, br)][:].rearrange("p (c m r) -> p r c m", c=2, m=16, r=16),
                 in1=bias[:, br],
                 op=ADD,
             )
-            left[n] = left[n] - 1
-            if n == NCH - 1:
-                if br == 1:
-                    nc.sync.dma_start(
-                        out=out_v[n][:, i % SUB, :],
-                        in_=obs[n][:, i % SUB].rearrange("p r b c m -> p (r b c m)"),
-                    )
-            elif left[n] == 0:
-                nc.sync.dma_start(
-                    out=out_v[n], in_=obs[n][:].rearrange("p t r b c m -> p t (r b c m)")
-                )
+
+        def evacuate(i, br):
+            part = obs[i // SUB][:, i % SUB, :, br]
+            nc.scalar.copy(
+                out=part, in_=accs[(i, br)][:].rearrange("p (c m r) -> p r c m", c=2, m=16, r=16)
+            )
+            nc.gpsimd.tensor_tensor(out=part, in0=part, in1=bias[:, br], op=ADD)
 
         ident = const.tile([P, P], F32)
         make_identity(nc, ident[:])
@@ -184,16 +170,16 @@ def tile_switchnet_fstar_pa_t_kernel(tc, x, k1, b1, out):
         w_piece(0, 1, 0, False)
         w_quantise(0, 0)
         w_quantise(0, 1)
-        for k in range(LEAD):
-            transposes(k)
-            copy_out(k)
+        transposes(0)
+        copy_out(0)
+        transposes(1)
+        copy_out(1)
+        load(XBUFS)
         w_piece(1, 1, 1, True)
         quantise(0)
-        quantise(1)
         w_piece(1, 0, 0, False)
         w_piece(1, 0, 1, False)
-        quantise(2)
-        quantise(3)
+        quantise(1)
         w_piece(1, 1, 0, False)
         w_quantise(1, 0)
         w_quantise(1, 1)
@@ -206,17 +192,37 @@ def tile_switchnet_fstar_pa_t_kernel(tc, x, k1, b1, out):
                 out=bias[:, br], in_=pb[:].rearrange("p (c m r) -> p r c m", c=2, m=16, r=16)
             )
 
-        order = [0, 2, 1, 3] + list(range(4, NBANK))
-        for k0 in range(0, NBANK, RUN):
-            ahead = list(range(LEAD + k0, min(LEAD + k0 + RUN, NBANK)))
-            now = order[k0 : k0 + RUN]
-            for k in ahead:
-                transposes(k)
-                copy_out(k)
-            for k in now:
-                multiply(k)
-            for j in range(RUN):
-                if j < len(now):
-                    add_bias(now[j])
-                if j < len(ahead):
-                    quantise(ahead[j])
+        for i in range(NSUB):
+            n = i // SUB
+            if i + LAG < NSUB:
+                transposes(i + LAG)
+                copy_out(i + LAG)
+                if (i + LAG) % SUB == SUB - 1 and (i + LAG) // SUB + XBUFS < NCH:
+                    load((i + LAG) // SUB + XBUFS)
+            if i == 0:
+                pairs = [(0, 0), (1, 0)]
+            elif i == 1:
+                pairs = [(0, 1), (1, 1)]
+            else:
+                pairs = [(i, 0), (i, 1)]
+            if i % SUB == 0:
+                ob = outs.tile([P, SUB, 16, 2, 2, 16], F32)
+                obs[n] = ob
+            for j, br in pairs:
+                multiply(j, br)
+            for j, br in pairs:
+                if br == 1 and j % SUB == 1 and 3 <= j <= 25:
+                    evacuate(j, br)
+                else:
+                    add_bias(j, br)
+            if i + LAG < NSUB:
+                quantise(i + LAG)
+            if n == NCH - 1:
+                nc.sync.dma_start(
+                    out=out_v[n][:, i % SUB, :],
+                    in_=obs[n][:, i % SUB].rearrange("p r b c m -> p (r b c m)"),
+                )
+            elif i % SUB == SUB - 1:
+                nc.sync.dma_start(
+                    out=out_v[n], in_=obs[n][:].rearrange("p t r b c m -> p t (r b c m)")
+                )

@@ -30,6 +30,7 @@ def tile_switchnet_fstar_pa_t_kernel(tc, x, k1, b1, out):
     with ExitStack() as ctx:
         const = ctx.enter_context(tc.tile_pool(name="const", bufs=1))
         xin = ctx.enter_context(tc.tile_pool(name="xin", bufs=XBUFS))
+        xre = ctx.enter_context(tc.tile_pool(name="xre", bufs=4))
         grp = ctx.enter_context(tc.tile_pool(name="grp", bufs=4))
         cod = ctx.enter_context(tc.tile_pool(name="cod", bufs=LAG + 3))
         outs = ctx.enter_context(tc.tile_pool(name="outs", bufs=4))
@@ -38,6 +39,7 @@ def tile_switchnet_fstar_pa_t_kernel(tc, x, k1, b1, out):
         ctx.enter_context(tc.manual_schedule())
 
         x_tiles = {}
+        sorted_words = {}
         banks = {}
         groups = {}
         codes = {}
@@ -54,13 +56,28 @@ def tile_switchnet_fstar_pa_t_kernel(tc, x, k1, b1, out):
                 nc.gpsimd.dma_start(out=xs[:].rearrange("p (t e) -> p t e", t=SUB), in_=x_v[n])
             x_tiles[n] = xs
 
+        def sort_words(i):
+            w0 = (i % SUB) * 1024 + 512
+            xs = xre.tile([P, 512], F32)
+            nc.scalar.copy(
+                out=xs[:].rearrange("p (c r w) -> p c r w", c=2, r=16, w=16),
+                in_=x_tiles[i // SUB][:]
+                .bitcast(F32)[:, w0 : w0 + 512]
+                .rearrange("p (r c w) -> p c r w", r=16, c=2, w=16),
+            )
+            sorted_words[i] = xs
+
         def transposes(i):
             xw = x_tiles[i // SUB][:].bitcast(F32)
             for br in range(2):
                 ps = psx.tile([P, 4, P], F32, tag="xt")
                 for u in range(4):
-                    c0 = (i % SUB) * 1024 + br * 512 + u * P
-                    nc.tensor.transpose(ps[:, u, :], xw[:, c0 : c0 + P], ident[:])
+                    if br == 0:
+                        c0 = (i % SUB) * 1024 + u * P
+                        words = xw[:, c0 : c0 + P]
+                    else:
+                        words = sorted_words[i][:, u * P : (u + 1) * P]
+                    nc.tensor.transpose(ps[:, u, :], words, ident[:])
                 banks[(i, br)] = ps
 
         def copy_out(i):
@@ -83,15 +100,18 @@ def tile_switchnet_fstar_pa_t_kernel(tc, x, k1, b1, out):
             acc = psa.tile([P, 512], F32, tag="acc")
             for s in range(2):
                 c0 = (br * 2 + s) * P
-                w0 = (br * 2 + s) * 512
+                if br == 0:
+                    w0, width, o0 = s * 512, 512, 0
+                else:
+                    w0, width, o0 = 1024 + s * 256, 256, s * 256
                 nc.tensor.matmul_mx(
-                    out=acc[:],
+                    out=acc[:, o0 : o0 + width],
                     lhsT=codes[i][:, c0 : c0 + P].bitcast(FP8X4),
                     lhsT_scale=planes[i][:, c0 : c0 + P],
-                    rhs=wc[:, w0 : w0 + 512].bitcast(FP8X4),
-                    rhs_scale=wp[:, w0 : w0 + 512],
-                    start=(s == 0),
-                    stop=(s == 1),
+                    rhs=wc[:, w0 : w0 + width].bitcast(FP8X4),
+                    rhs_scale=wp[:, w0 : w0 + width],
+                    start=(br == 1 or s == 0),
+                    stop=(br == 1 or s == 1),
                 )
             accs[(i, br)] = acc
 
@@ -103,30 +123,27 @@ def tile_switchnet_fstar_pa_t_kernel(tc, x, k1, b1, out):
                 op=ADD,
             )
 
-        def evacuate(i, br):
-            part = obs[i // SUB][:, i % SUB, :, br]
-            nc.scalar.copy(
-                out=part, in_=accs[(i, br)][:].rearrange("p (c m r) -> p r c m", c=2, m=16, r=16)
-            )
-            nc.gpsimd.tensor_tensor(out=part, in0=part, in1=bias[:, br], op=ADD)
-
         ident = const.tile([P, P], F32)
         make_identity(nc, ident[:])
         for n in range(XBUFS):
             load(n)
 
-        wraw = const.tile([P, 2, 8, 256], BF16)
-        for br in range(2):
-            for r in (0, 2, 1, 3):
-                for bc in range(2):
-                    p0 = r * 32 + bc * 16
-                    src = k1[br * 2 + bc].rearrange(
-                        "(u r c h) l -> r c u (h l)", u=4, r=4, c=16, h=2
-                    )[r]
-                    queue = nc.sync if bc == 0 else nc.scalar
-                    queue.dma_start(
-                        out=wraw[p0 : p0 + 16, br].rearrange("p (u h) l -> p u (h l)", h=2), in_=src
-                    )
+        wraw1 = const.tile([P, 2, 4, 256], BF16)
+        for bc in range(2):
+            queue = nc.sync if bc == 0 else nc.scalar
+            queue.dma_start(
+                out=wraw1[:, bc].rearrange("p (u h) l -> p u (h l)", h=2),
+                in_=k1[2 + bc].rearrange("(u p h) l -> p u (h l)", u=2, p=P, h=2),
+            )
+        wraw0 = const.tile([P, 8, 256], BF16)
+        for r in (0, 2, 1, 3):
+            for bc in range(2):
+                p0 = r * 32 + bc * 16
+                src = k1[bc].rearrange("(u r c h) l -> r c u (h l)", u=4, r=4, c=16, h=2)[r]
+                queue = nc.sync if bc == 0 else nc.scalar
+                queue.dma_start(
+                    out=wraw0[p0 : p0 + 16].rearrange("p (u h) l -> p u (h l)", h=2), in_=src
+                )
         brow = const.tile([P, 1024], BF16)
         nc.vector.memset(brow[:], 0.0)
         nc.sync.dma_start(out=brow[0:1, :], in_=b1.rearrange("o j l -> o (j l)"))
@@ -141,13 +158,13 @@ def tile_switchnet_fstar_pa_t_kernel(tc, x, k1, b1, out):
         )
         bias = const.tile([P, 2, 16, 2, 16], F32)
 
-        wg = const.tile([P, 4 * 2048], BF16, align_bytes=64)
-        wc = const.tile([P, 4 * 512], U32, align_bytes=64)
-        wp = const.tile([P, 4 * 512], U8, align_bytes=64)
+        wg = const.tile([P, 3 * 2048], BF16, align_bytes=64)
+        wc = const.tile([P, 3 * 512], U32, align_bytes=64)
+        wp = const.tile([P, 3 * 512], U8, align_bytes=64)
 
-        def w_piece(br, s, bcc, on_scalar):
-            o0 = (br * 2 + s) * 2048 + bcc * 1024
-            src = wraw[:, br, 4 * s : 4 * s + 4, :].rearrange("p t (c i) -> p c t i", i=4)
+        def w_piece(s, bcc, on_scalar):
+            o0 = s * 2048 + bcc * 1024
+            src = wraw0[:, 4 * s : 4 * s + 4, :].rearrange("p t (c i) -> p c t i", i=4)
             dst = wg[:, o0 : o0 + 1024].rearrange("p (c i t) -> p c t i", i=4, t=4)
             if on_scalar:
                 nc.scalar.activation(out=dst, in_=src, func=COPY, scale=mask[:, bcc : bcc + 1])
@@ -156,33 +173,39 @@ def tile_switchnet_fstar_pa_t_kernel(tc, x, k1, b1, out):
                     out=dst, in0=src, scalar1=mask[:, bcc : bcc + 1], scalar2=None, op0=MULT
                 )
 
-        def w_quantise(br, s):
-            q = br * 2 + s
+        def w_dense(bc):
+            o0 = 4096 + bc * 1024
+            nc.vector.tensor_copy(
+                out=wg[:, o0 : o0 + 1024].rearrange("p (c i t) -> p c t i", i=4, t=4),
+                in_=wraw1[:, bc].rearrange("p t (c i) -> p c t i", i=4),
+            )
+
+        def w_quantise(q):
             nc.vector.quantize_mx(
                 out=wc[:, q * 512 : (q + 1) * 512].bitcast(FP8X4),
                 scales=wp[:, q * 512 : (q + 1) * 512],
                 in_=wg[:, q * 2048 : (q + 1) * 2048],
             )
 
-        w_piece(0, 1, 1, True)
-        w_piece(0, 0, 0, False)
-        w_piece(0, 0, 1, False)
-        w_piece(0, 1, 0, False)
-        w_quantise(0, 0)
-        w_quantise(0, 1)
+        w_dense(0)
+        w_dense(1)
+        sort_words(0)
         transposes(0)
         copy_out(0)
+        w_quantise(2)
+        sort_words(1)
         transposes(1)
-        copy_out(1)
-        load(XBUFS)
-        w_piece(1, 1, 1, True)
+        w_piece(0, 0, False)
         quantise(0)
-        w_piece(1, 0, 0, False)
-        w_piece(1, 0, 1, False)
+        w_piece(0, 1, False)
+        copy_out(1)
+        w_piece(1, 1, True)
+        sort_words(2)
+        load(XBUFS)
+        w_piece(1, 0, False)
+        w_quantise(0)
         quantise(1)
-        w_piece(1, 1, 0, False)
-        w_quantise(1, 0)
-        w_quantise(1, 1)
+        w_quantise(1)
         for br in range(2):
             pb = psa.tile([P, 512], F32, tag="acc")
             nc.tensor.matmul(
@@ -197,12 +220,14 @@ def tile_switchnet_fstar_pa_t_kernel(tc, x, k1, b1, out):
             if i + LAG < NSUB:
                 transposes(i + LAG)
                 copy_out(i + LAG)
+                if i + LAG + 1 < NSUB:
+                    sort_words(i + LAG + 1)
                 if (i + LAG) % SUB == SUB - 1 and (i + LAG) // SUB + XBUFS < NCH:
                     load((i + LAG) // SUB + XBUFS)
             if i == 0:
-                pairs = [(0, 0), (1, 0)]
-            elif i == 1:
                 pairs = [(0, 1), (1, 1)]
+            elif i == 1:
+                pairs = [(0, 0), (1, 0)]
             else:
                 pairs = [(i, 0), (i, 1)]
             if i % SUB == 0:
@@ -211,10 +236,7 @@ def tile_switchnet_fstar_pa_t_kernel(tc, x, k1, b1, out):
             for j, br in pairs:
                 multiply(j, br)
             for j, br in pairs:
-                if br == 1 and j % SUB == 1 and 3 <= j <= 25:
-                    evacuate(j, br)
-                else:
-                    add_bias(j, br)
+                add_bias(j, br)
             if i + LAG < NSUB:
                 quantise(i + LAG)
             if n == NCH - 1:

@@ -30,7 +30,7 @@ def tile_switchnet_fstar_pa_t_kernel(tc, x, k1, b1, out):
     with ExitStack() as ctx:
         const = ctx.enter_context(tc.tile_pool(name="const", bufs=1))
         xin = ctx.enter_context(tc.tile_pool(name="xin", bufs=XBUFS))
-        xre = ctx.enter_context(tc.tile_pool(name="xre", bufs=4))
+        xre = ctx.enter_context(tc.tile_pool(name="xre", bufs=5))
         grp = ctx.enter_context(tc.tile_pool(name="grp", bufs=4))
         cod = ctx.enter_context(tc.tile_pool(name="cod", bufs=LAG + 3))
         outs = ctx.enter_context(tc.tile_pool(name="outs", bufs=4))
@@ -201,6 +201,7 @@ def tile_switchnet_fstar_pa_t_kernel(tc, x, k1, b1, out):
         copy_out(1)
         w_piece(1, 1, True)
         sort_words(2)
+        sort_words(3)
         load(XBUFS)
         w_piece(1, 0, False)
         w_quantise(0)
@@ -220,8 +221,8 @@ def tile_switchnet_fstar_pa_t_kernel(tc, x, k1, b1, out):
             if i + LAG < NSUB:
                 transposes(i + LAG)
                 copy_out(i + LAG)
-                if i + LAG + 1 < NSUB:
-                    sort_words(i + LAG + 1)
+                if i + LAG + 2 < NSUB:
+                    sort_words(i + LAG + 2)
                 if (i + LAG) % SUB == SUB - 1 and (i + LAG) // SUB + XBUFS < NCH:
                     load((i + LAG) // SUB + XBUFS)
             if i == 0:

@@ -12,7 +12,6 @@ U8 = mybir.dt.uint8
 FP8X4 = mybir.dt.float8_e4m3fn_x4
 ADD = mybir.AluOpType.add
 MULT = mybir.AluOpType.mult
-COPY = mybir.ActivationFunctionType.Copy
 
 P = 128
 SUB = 2
@@ -47,13 +46,13 @@ def tile_switchnet_fstar_pa_t_kernel(tc, x, k1, b1, out):
         accs = {}
         obs = {}
 
-        def load(n):
+        def load(n, queue):
             xs = xin.tile([P, SUB * 2048], BF16)
             if n == 0:
                 for t in range(SUB):
-                    nc.gpsimd.dma_start(out=xs[:, t * 2048 : (t + 1) * 2048], in_=x_v[n][:, t, :])
+                    queue.dma_start(out=xs[:, t * 2048 : (t + 1) * 2048], in_=x_v[n][:, t, :])
             else:
-                nc.gpsimd.dma_start(out=xs[:].rearrange("p (t e) -> p t e", t=SUB), in_=x_v[n])
+                queue.dma_start(out=xs[:].rearrange("p (t e) -> p t e", t=SUB), in_=x_v[n])
             x_tiles[n] = xs
 
         def sort_words(i):
@@ -123,30 +122,29 @@ def tile_switchnet_fstar_pa_t_kernel(tc, x, k1, b1, out):
                 op=ADD,
             )
 
-        ident = const.tile([P, P], F32)
-        make_identity(nc, ident[:])
-        for n in range(XBUFS):
-            load(n)
-
-        wraw1 = const.tile([P, 2, 4, 256], BF16)
-        for bc in range(2):
-            queue = nc.sync if bc == 0 else nc.scalar
-            queue.dma_start(
-                out=wraw1[:, bc].rearrange("p (u h) l -> p u (h l)", h=2),
-                in_=k1[2 + bc].rearrange("(u p h) l -> p u (h l)", u=2, p=P, h=2),
-            )
+        load(0, nc.gpsimd)
+        wraw1 = const.tile([P, 4, 512], BF16)
+        nc.sync.dma_start(
+            out=wraw1[:], in_=k1[2:4].rearrange("j (u p h) l -> p (j u) (h l)", u=2, p=P, h=2)
+        )
+        brow = const.tile([P, 1024], BF16)
+        nc.vector.memset(brow[:], 0.0)
+        nc.scalar.dma_start(out=brow[0:1, :], in_=b1.rearrange("o j l -> o (j l)"))
         wraw0 = const.tile([P, 8, 256], BF16)
         for r in (0, 2, 1, 3):
             for bc in range(2):
                 p0 = r * 32 + bc * 16
                 src = k1[bc].rearrange("(u r c h) l -> r c u (h l)", u=4, r=4, c=16, h=2)[r]
-                queue = nc.sync if bc == 0 else nc.scalar
+                queue = nc.scalar if bc == 1 and r != 3 else nc.sync
                 queue.dma_start(
                     out=wraw0[p0 : p0 + 16].rearrange("p (u h) l -> p u (h l)", h=2), in_=src
                 )
-        brow = const.tile([P, 1024], BF16)
-        nc.vector.memset(brow[:], 0.0)
-        nc.sync.dma_start(out=brow[0:1, :], in_=b1.rearrange("o j l -> o (j l)"))
+        load(1, nc.sync)
+        ident = const.tile([P, P], F32)
+        make_identity(nc, ident[:])
+        for n in range(2, XBUFS):
+            load(n, nc.gpsimd)
+
         ones = const.tile([P, P], BF16)
         nc.vector.memset(ones[:], 1.0)
         mask = const.tile([P, 2], F32)
@@ -157,27 +155,36 @@ def tile_switchnet_fstar_pa_t_kernel(tc, x, k1, b1, out):
             op=ADD,
         )
         bias = const.tile([P, 2, 16, 2, 16], F32)
+        for br in range(2):
+            pb = psa.tile([P, 512], F32, tag="acc")
+            nc.tensor.matmul(
+                pb[:], lhsT=ones[:], rhs=brow[:, br * 512 : (br + 1) * 512], start=True, stop=True
+            )
+            nc.scalar.copy(
+                out=bias[:, br], in_=pb[:].rearrange("p (c m r) -> p r c m", c=2, m=16, r=16)
+            )
 
         wg = const.tile([P, 3 * 2048], BF16, align_bytes=64)
         wc = const.tile([P, 3 * 512], U32, align_bytes=64)
         wp = const.tile([P, 3 * 512], U8, align_bytes=64)
 
-        def w_piece(s, bcc, on_scalar):
+        def w_piece(s, bcc):
             o0 = s * 2048 + bcc * 1024
-            src = wraw0[:, 4 * s : 4 * s + 4, :].rearrange("p t (c i) -> p c t i", i=4)
-            dst = wg[:, o0 : o0 + 1024].rearrange("p (c i t) -> p c t i", i=4, t=4)
-            if on_scalar:
-                nc.scalar.activation(out=dst, in_=src, func=COPY, scale=mask[:, bcc : bcc + 1])
-            else:
-                nc.vector.tensor_scalar(
-                    out=dst, in0=src, scalar1=mask[:, bcc : bcc + 1], scalar2=None, op0=MULT
-                )
+            nc.vector.tensor_scalar(
+                out=wg[:, o0 : o0 + 1024].rearrange("p (c i t) -> p c t i", i=4, t=4),
+                in0=wraw0[:, 4 * s : 4 * s + 4, :].rearrange("p t (c i) -> p c t i", i=4),
+                scalar1=mask[:, bcc : bcc + 1],
+                scalar2=None,
+                op0=MULT,
+            )
 
         def w_dense(bc):
             o0 = 4096 + bc * 1024
             nc.vector.tensor_copy(
                 out=wg[:, o0 : o0 + 1024].rearrange("p (c i t) -> p c t i", i=4, t=4),
-                in_=wraw1[:, bc].rearrange("p t (c i) -> p c t i", i=4),
+                in_=wraw1[:, 2 * bc : 2 * bc + 2, :].rearrange(
+                    "p u (h c i) -> p c (u h) i", h=2, i=4
+                ),
             )
 
         def w_quantise(q):
@@ -189,32 +196,22 @@ def tile_switchnet_fstar_pa_t_kernel(tc, x, k1, b1, out):
 
         w_dense(0)
         w_dense(1)
+        w_quantise(2)
         sort_words(0)
         transposes(0)
         copy_out(0)
-        w_quantise(2)
         sort_words(1)
         transposes(1)
-        w_piece(0, 0, False)
-        quantise(0)
-        w_piece(0, 1, False)
         copy_out(1)
-        w_piece(1, 1, True)
+        for s in range(2):
+            for bcc in range(2):
+                w_piece(s, bcc)
+            w_quantise(s)
+        quantise(0)
         sort_words(2)
         sort_words(3)
-        load(XBUFS)
-        w_piece(1, 0, False)
-        w_quantise(0)
+        load(XBUFS, nc.gpsimd)
         quantise(1)
-        w_quantise(1)
-        for br in range(2):
-            pb = psa.tile([P, 512], F32, tag="acc")
-            nc.tensor.matmul(
-                pb[:], lhsT=ones[:], rhs=brow[:, br * 512 : (br + 1) * 512], start=True, stop=True
-            )
-            nc.scalar.copy(
-                out=bias[:, br], in_=pb[:].rearrange("p (c m r) -> p r c m", c=2, m=16, r=16)
-            )
 
         for i in range(NSUB):
             n = i // SUB
@@ -224,7 +221,7 @@ def tile_switchnet_fstar_pa_t_kernel(tc, x, k1, b1, out):
                 if i + LAG + 2 < NSUB:
                     sort_words(i + LAG + 2)
                 if (i + LAG) % SUB == SUB - 1 and (i + LAG) // SUB + XBUFS < NCH:
-                    load((i + LAG) // SUB + XBUFS)
+                    load((i + LAG) // SUB + XBUFS, nc.gpsimd)
             if i == 0:
                 pairs = [(0, 1), (1, 1)]
             elif i == 1:

@@ -32,7 +32,7 @@ def tile_switchnet_fstar_pa_t_kernel(tc, x, k1, b1, out):
         xre = ctx.enter_context(tc.tile_pool(name="xre", bufs=5))
         grp = ctx.enter_context(tc.tile_pool(name="grp", bufs=4))
         cod = ctx.enter_context(tc.tile_pool(name="cod", bufs=LAG + 3))
-        outs = ctx.enter_context(tc.tile_pool(name="outs", bufs=4))
+        outs = ctx.enter_context(tc.tile_pool(name="outs", bufs=10))
         psx = ctx.enter_context(tc.psum_pool(name="psx", bufs=4))
         psa = ctx.enter_context(tc.psum_pool(name="psa", bufs=4))
         ctx.enter_context(tc.manual_schedule())
@@ -147,13 +147,6 @@ def tile_switchnet_fstar_pa_t_kernel(tc, x, k1, b1, out):
 
         ones = const.tile([P, P], BF16)
         nc.vector.memset(ones[:], 1.0)
-        mask = const.tile([P, 2], F32)
-        nc.vector.tensor_reduce(
-            out=mask[:],
-            in_=ident[:].rearrange("p (g h c) -> p h g c", g=4, h=2, c=16),
-            axis=mybir.AxisListType.XY,
-            op=ADD,
-        )
         bias = const.tile([P, 2, 16, 2, 16], F32)
         for br in range(2):
             pb = psa.tile([P, 512], F32, tag="acc")
@@ -164,6 +157,7 @@ def tile_switchnet_fstar_pa_t_kernel(tc, x, k1, b1, out):
                 out=bias[:, br], in_=pb[:].rearrange("p (c m r) -> p r c m", c=2, m=16, r=16)
             )
 
+        mask = const.tile([P, 2], F32)
         wg = const.tile([P, 3 * 2048], BF16, align_bytes=64)
         wc = const.tile([P, 3 * 512], U32, align_bytes=64)
         wp = const.tile([P, 3 * 512], U8, align_bytes=64)
@@ -197,6 +191,12 @@ def tile_switchnet_fstar_pa_t_kernel(tc, x, k1, b1, out):
         w_dense(0)
         w_dense(1)
         w_quantise(2)
+        nc.vector.tensor_reduce(
+            out=mask[:],
+            in_=ident[:].rearrange("p (g h c) -> p h g c", g=4, h=2, c=16),
+            axis=mybir.AxisListType.XY,
+            op=ADD,
+        )
         sort_words(0)
         transposes(0)
         copy_out(0)

@@ -143,7 +143,7 @@ def tile_switchnet_fstar_pa_t_kernel(tc, x, k1, b1, out):
         ident = const.tile([P, P], F32)
         make_identity(nc, ident[:])
         for n in range(2, XBUFS):
-            load(n, nc.gpsimd)
+            load(n, nc.sync)
 
         ones = const.tile([P, P], BF16)
         nc.vector.memset(ones[:], 1.0)
@@ -210,7 +210,7 @@ def tile_switchnet_fstar_pa_t_kernel(tc, x, k1, b1, out):
         quantise(0)
         sort_words(2)
         sort_words(3)
-        load(XBUFS, nc.gpsimd)
+        load(XBUFS, nc.sync)
         quantise(1)
 
         for i in range(NSUB):
@@ -221,7 +221,7 @@ def tile_switchnet_fstar_pa_t_kernel(tc, x, k1, b1, out):
                 if i + LAG + 2 < NSUB:
                     sort_words(i + LAG + 2)
                 if (i + LAG) % SUB == SUB - 1 and (i + LAG) // SUB + XBUFS < NCH:
-                    load((i + LAG) // SUB + XBUFS, nc.gpsimd)
+                    load((i + LAG) // SUB + XBUFS, nc.sync)
             if i == 0:
                 pairs = [(0, 1), (1, 1)]
             elif i == 1:

@@ -14,10 +14,10 @@ ADD = mybir.AluOpType.add
 MULT = mybir.AluOpType.mult
 
 P = 128
-SUB = 2
+SUB = 4
 NCH = 4096 // (P * SUB)
 NSUB = NCH * SUB
-XBUFS = 8
+XBUFS = 5
 LAG = 2
 
 
@@ -32,7 +32,7 @@ def tile_switchnet_fstar_pa_t_kernel(tc, x, k1, b1, out):
         xre = ctx.enter_context(tc.tile_pool(name="xre", bufs=5))
         grp = ctx.enter_context(tc.tile_pool(name="grp", bufs=4))
         cod = ctx.enter_context(tc.tile_pool(name="cod", bufs=LAG + 3))
-        outs = ctx.enter_context(tc.tile_pool(name="outs", bufs=10))
+        outs = ctx.enter_context(tc.tile_pool(name="outs", bufs=5))
         psx = ctx.enter_context(tc.psum_pool(name="psx", bufs=4))
         psa = ctx.enter_context(tc.psum_pool(name="psa", bufs=4))
         ctx.enter_context(tc.manual_schedule())
@@ -46,13 +46,17 @@ def tile_switchnet_fstar_pa_t_kernel(tc, x, k1, b1, out):
         accs = {}
         obs = {}
 
-        def load(n, queue):
+        def load(n):
             xs = xin.tile([P, SUB * 2048], BF16)
             if n == 0:
-                for t in range(SUB):
-                    queue.dma_start(out=xs[:, t * 2048 : (t + 1) * 2048], in_=x_v[n][:, t, :])
+                for t0, t1 in ((0, 1), (1, 2), (2, SUB)):
+                    queue = nc.gpsimd if t0 == 0 else nc.sync
+                    queue.dma_start(
+                        out=xs[:, t0 * 2048 : t1 * 2048].rearrange("p (t e) -> p t e", e=2048),
+                        in_=x_v[n][:, t0:t1, :],
+                    )
             else:
-                queue.dma_start(out=xs[:].rearrange("p (t e) -> p t e", t=SUB), in_=x_v[n])
+                nc.sync.dma_start(out=xs[:].rearrange("p (t e) -> p t e", t=SUB), in_=x_v[n])
             x_tiles[n] = xs
 
         def sort_words(i):
@@ -114,21 +118,23 @@ def tile_switchnet_fstar_pa_t_kernel(tc, x, k1, b1, out):
                 )
             accs[(i, br)] = acc
 
-        def add_bias(i, br):
+        def add_bias(i, br, half):
+            r = slice(0, 16) if half is None else slice(8 * half, 8 * half + 8)
             nc.vector.tensor_tensor(
-                out=obs[i // SUB][:, i % SUB, :, br],
-                in0=accs[(i, br)][:].rearrange("p (c m r) -> p r c m", c=2, m=16, r=16),
-                in1=bias[:, br],
+                out=obs[i // SUB][:, i % SUB, r, br],
+                in0=accs[(i, br)][:].rearrange("p (c m r) -> p r c m", c=2, m=16, r=16)[:, r],
+                in1=bias[:, br, r],
                 op=ADD,
             )
 
-        load(0, nc.gpsimd)
+        ident = const.tile([P, P], F32)
+        make_identity(nc, ident[:])
+        brow = const.tile([P, 1024], BF16)
+        nc.vector.memset(brow[:].bitcast(F32), 0.0)
         wraw1 = const.tile([P, 4, 512], BF16)
         nc.sync.dma_start(
             out=wraw1[:], in_=k1[2:4].rearrange("j (u p h) l -> p (j u) (h l)", u=2, p=P, h=2)
         )
-        brow = const.tile([P, 1024], BF16)
-        nc.vector.memset(brow[:], 0.0)
         nc.scalar.dma_start(out=brow[0:1, :], in_=b1.rearrange("o j l -> o (j l)"))
         wraw0 = const.tile([P, 8, 256], BF16)
         for r in (0, 2, 1, 3):
@@ -139,25 +145,21 @@ def tile_switchnet_fstar_pa_t_kernel(tc, x, k1, b1, out):
                 queue.dma_start(
                     out=wraw0[p0 : p0 + 16].rearrange("p (u h) l -> p u (h l)", h=2), in_=src
                 )
-        load(1, nc.sync)
-        ident = const.tile([P, P], F32)
-        make_identity(nc, ident[:])
-        for n in range(2, XBUFS):
-            load(n, nc.sync)
-
-        ones = const.tile([P, P], BF16)
-        nc.vector.memset(ones[:], 1.0)
-        bias = const.tile([P, 2, 16, 2, 16], F32)
-        for br in range(2):
-            pb = psa.tile([P, 512], F32, tag="acc")
-            nc.tensor.matmul(
-                pb[:], lhsT=ones[:], rhs=brow[:, br * 512 : (br + 1) * 512], start=True, stop=True
-            )
-            nc.scalar.copy(
-                out=bias[:, br], in_=pb[:].rearrange("p (c m r) -> p r c m", c=2, m=16, r=16)
-            )
+        for n in range(XBUFS):
+            load(n)
 
         mask = const.tile([P, 2], F32)
+        nc.vector.tensor_reduce(
+            out=mask[:],
+            in_=ident[:].rearrange("p (g h c) -> p h g c", g=4, h=2, c=16),
+            axis=mybir.AxisListType.XY,
+            op=ADD,
+        )
+        ones = const.tile([P, P], BF16)
+        nc.vector.memset(ones[:], 1.0)
+        warm = const.tile([P, 2], F32)
+        nc.scalar.copy(out=warm[:], in_=mask[:])
+        bias = const.tile([P, 2, 16, 2, 16], F32)
         wg = const.tile([P, 3 * 2048], BF16, align_bytes=64)
         wc = const.tile([P, 3 * 512], U32, align_bytes=64)
         wp = const.tile([P, 3 * 512], U8, align_bytes=64)
@@ -191,12 +193,14 @@ def tile_switchnet_fstar_pa_t_kernel(tc, x, k1, b1, out):
         w_dense(0)
         w_dense(1)
         w_quantise(2)
-        nc.vector.tensor_reduce(
-            out=mask[:],
-            in_=ident[:].rearrange("p (g h c) -> p h g c", g=4, h=2, c=16),
-            axis=mybir.AxisListType.XY,
-            op=ADD,
-        )
+        for br in range(2):
+            pb = psa.tile([P, 512], F32, tag="acc")
+            nc.tensor.matmul(
+                pb[:], lhsT=ones[:], rhs=brow[:, br * 512 : (br + 1) * 512], start=True, stop=True
+            )
+            nc.scalar.copy(
+                out=bias[:, br], in_=pb[:].rearrange("p (c m r) -> p r c m", c=2, m=16, r=16)
+            )
         sort_words(0)
         transposes(0)
         copy_out(0)
@@ -208,10 +212,9 @@ def tile_switchnet_fstar_pa_t_kernel(tc, x, k1, b1, out):
                 w_piece(s, bcc)
             w_quantise(s)
         quantise(0)
+        quantise(1)
         sort_words(2)
         sort_words(3)
-        load(XBUFS, nc.sync)
-        quantise(1)
 
         for i in range(NSUB):
             n = i // SUB
@@ -221,28 +224,29 @@ def tile_switchnet_fstar_pa_t_kernel(tc, x, k1, b1, out):
                 if i + LAG + 2 < NSUB:
                     sort_words(i + LAG + 2)
                 if (i + LAG) % SUB == SUB - 1 and (i + LAG) // SUB + XBUFS < NCH:
-                    load((i + LAG) // SUB + XBUFS, nc.sync)
-            if i == 0:
-                pairs = [(0, 1), (1, 1)]
-            elif i == 1:
-                pairs = [(0, 0), (1, 0)]
-            else:
-                pairs = [(i, 0), (i, 1)]
+                    load((i + LAG) // SUB + XBUFS)
             if i % SUB == 0:
                 ob = outs.tile([P, SUB, 16, 2, 2, 16], F32)
                 obs[n] = ob
-            for j, br in pairs:
-                multiply(j, br)
-            for j, br in pairs:
-                add_bias(j, br)
+            for br in range(2):
+                multiply(i, br)
+            for h in range(2) if i == NSUB - 1 else [None]:
+                for br in range(2):
+                    add_bias(i, br, h)
+                if h is not None:
+                    nc.sync.dma_start(
+                        out=out_v[n][:, i % SUB, h * 512 : (h + 1) * 512],
+                        in_=obs[n][:, i % SUB, 8 * h : 8 * h + 8].rearrange("p r b c m -> p (r b c m)"),
+                    )
             if i + LAG < NSUB:
                 quantise(i + LAG)
-            if n == NCH - 1:
+            if i < NSUB - SUB:
+                done = (0, SUB) if i % SUB == SUB - 1 else None
+            else:
+                done = {1: (0, 2), 2: (2, 3)}.get(i % SUB)
+            if done is not None:
+                t0, t1 = done
                 nc.sync.dma_start(
-                    out=out_v[n][:, i % SUB, :],
-                    in_=obs[n][:, i % SUB].rearrange("p r b c m -> p (r b c m)"),
-                )
-            elif i % SUB == SUB - 1:
-                nc.sync.dma_start(
-                    out=out_v[n], in_=obs[n][:].rearrange("p t r b c m -> p t (r b c m)")
+                    out=out_v[n][:, t0:t1, :],
+                    in_=obs[n][:, t0:t1].rearrange("p t r b c m -> p t (r b c m)"),
                 )

@@ -11,7 +11,6 @@ U32 = mybir.dt.uint32
 U8 = mybir.dt.uint8
 FP8X4 = mybir.dt.float8_e4m3fn_x4
 ADD = mybir.AluOpType.add
-MULT = mybir.AluOpType.mult
 
 P = 128
 SUB = 4
@@ -50,8 +49,7 @@ def tile_switchnet_fstar_pa_t_kernel(tc, x, k1, b1, out):
             xs = xin.tile([P, SUB * 2048], BF16)
             if n == 0:
                 for t0, t1 in ((0, 1), (1, 2), (2, SUB)):
-                    queue = nc.gpsimd if t0 == 0 else nc.sync
-                    queue.dma_start(
+                    nc.sync.dma_start(
                         out=xs[:, t0 * 2048 : t1 * 2048].rearrange("p (t e) -> p t e", e=2048),
                         in_=x_v[n][:, t0:t1, :],
                     )
@@ -122,7 +120,9 @@ def tile_switchnet_fstar_pa_t_kernel(tc, x, k1, b1, out):
             r = slice(0, 16) if half is None else slice(8 * half, 8 * half + 8)
             nc.vector.tensor_tensor(
                 out=obs[i // SUB][:, i % SUB, r, br],
-                in0=accs[(i, br)][:].rearrange("p (c m r) -> p r c m", c=2, m=16, r=16)[:, r],
+                in0=accs[(i, br)][:].rearrange(
+                    "p (r c m) -> p r c m" if br == 0 else "p (c r m) -> p r c m", c=2, m=16, r=16
+                )[:, r],
                 in1=bias[:, br, r],
                 op=ADD,
             )
@@ -131,55 +131,63 @@ def tile_switchnet_fstar_pa_t_kernel(tc, x, k1, b1, out):
         make_identity(nc, ident[:])
         brow = const.tile([P, 1024], BF16)
         nc.vector.memset(brow[:].bitcast(F32), 0.0)
-        wraw1 = const.tile([P, 4, 512], BF16)
-        nc.sync.dma_start(
-            out=wraw1[:], in_=k1[2:4].rearrange("j (u p h) l -> p (j u) (h l)", u=2, p=P, h=2)
-        )
-        nc.scalar.dma_start(out=brow[0:1, :], in_=b1.rearrange("o j l -> o (j l)"))
-        wraw0 = const.tile([P, 8, 256], BF16)
-        for r in (0, 2, 1, 3):
-            for bc in range(2):
-                p0 = r * 32 + bc * 16
-                src = k1[bc].rearrange("(u r c h) l -> r c u (h l)", u=4, r=4, c=16, h=2)[r]
-                queue = nc.scalar if bc == 1 and r != 3 else nc.sync
-                queue.dma_start(
-                    out=wraw0[p0 : p0 + 16].rearrange("p (u h) l -> p u (h l)", h=2), in_=src
-                )
+        wraw = const.tile([P, 8, 512], BF16)
+        for br in (1, 0):
+            nc.sync.dma_start(
+                out=wraw[:, 4 * br : 4 * br + 4, :],
+                in_=k1[2 * br : 2 * br + 2].rearrange("j (u p h) l -> p (j u) (h l)", u=2, p=P, h=2),
+            )
+        nc.sync.dma_start(out=brow[0:1, :], in_=b1.rearrange("o j l -> o (j l)"))
         for n in range(XBUFS):
             load(n)
 
-        mask = const.tile([P, 2], F32)
-        nc.vector.tensor_reduce(
-            out=mask[:],
-            in_=ident[:].rearrange("p (g h c) -> p h g c", g=4, h=2, c=16),
-            axis=mybir.AxisListType.XY,
-            op=ADD,
-        )
+        place = const.tile([P, 2, 2, P], BF16)
+        nc.vector.memset(place[:].rearrange("p g b c -> p (g b c)").bitcast(F32), 0.0)
+        for g in range(2):
+            for bc in range(2):
+                nc.vector.tensor_copy(
+                    out=place[:, g, bc].rearrange("p (r b w) -> p r b w", r=4, b=2)[:, :, bc, :],
+                    in_=ident[:, g * 64 : (g + 1) * 64].rearrange("p (r w) -> p r w", r=4),
+                )
         ones = const.tile([P, P], BF16)
         nc.vector.memset(ones[:], 1.0)
         warm = const.tile([P, 2], F32)
-        nc.scalar.copy(out=warm[:], in_=mask[:])
+        nc.scalar.copy(out=warm[:], in_=ident[:, 0:2])
         bias = const.tile([P, 2, 16, 2, 16], F32)
         wg = const.tile([P, 3 * 2048], BF16, align_bytes=64)
         wc = const.tile([P, 3 * 512], U32, align_bytes=64)
         wp = const.tile([P, 3 * 512], U8, align_bytes=64)
 
-        def w_piece(s, bcc):
-            o0 = s * 2048 + bcc * 1024
-            nc.vector.tensor_scalar(
-                out=wg[:, o0 : o0 + 1024].rearrange("p (c i t) -> p c t i", i=4, t=4),
-                in0=wraw0[:, 4 * s : 4 * s + 4, :].rearrange("p t (c i) -> p c t i", i=4),
-                scalar1=mask[:, bcc : bcc + 1],
-                scalar2=None,
-                op0=MULT,
-            )
+        def w_piece(s, bc, half):
+            if s == 0:
+                xt = psx.tile([P, 4, P], F32, tag="xt")
+                bank = xt[:]
+            else:
+                acc = psa.tile([P, 512], F32, tag="acc")
+                bank = acc[:].rearrange("p (t c) -> p t c", t=4)
+            cols = slice(half * P, (half + 1) * P)
+            for g in range(2):
+                nc.tensor.matmul(
+                    bank[:, 2 * g : 2 * g + 2, :],
+                    lhsT=place[:, g, bc, :],
+                    rhs=wraw[:, 2 * bc + s, :].rearrange("p (h l) -> p h l", h=2)[:, :, cols],
+                    start=True,
+                    stop=True,
+                )
+            dst = wg[:, s * 2048 : (s + 1) * 2048].rearrange("p (r b m t) -> p r b m t", r=16, b=2, m=16)
+            dst = dst[:, :, bc, 8 * half : 8 * half + 8, :]
+            src = bank.rearrange("p t (m r) -> p r m t", r=16)
+            if half == 0:
+                nc.scalar.copy(out=dst, in_=src)
+            else:
+                nc.vector.tensor_copy(out=dst, in_=src)
 
         def w_dense(bc):
             o0 = 4096 + bc * 1024
             nc.vector.tensor_copy(
-                out=wg[:, o0 : o0 + 1024].rearrange("p (c i t) -> p c t i", i=4, t=4),
-                in_=wraw1[:, 2 * bc : 2 * bc + 2, :].rearrange(
-                    "p u (h c i) -> p c (u h) i", h=2, i=4
+                out=wg[:, o0 : o0 + 1024].rearrange("p (r m t) -> p r m t", r=16, t=4),
+                in_=wraw[:, 4 + 2 * bc : 6 + 2 * bc, :].rearrange(
+                    "p u (h m r) -> p r m (u h)", h=2, r=16
                 ),
             )
 
@@ -193,6 +201,17 @@ def tile_switchnet_fstar_pa_t_kernel(tc, x, k1, b1, out):
         w_dense(0)
         w_dense(1)
         w_quantise(2)
+        for s in range(2):
+            for bc in range(2):
+                for half in range(2):
+                    w_piece(s, bc, half)
+            w_quantise(s)
+            sort_words(s)
+            if s == 0:
+                transposes(0)
+        copy_out(0)
+        transposes(1)
+        copy_out(1)
         for br in range(2):
             pb = psa.tile([P, 512], F32, tag="acc")
             nc.tensor.matmul(
@@ -201,16 +220,6 @@ def tile_switchnet_fstar_pa_t_kernel(tc, x, k1, b1, out):
             nc.scalar.copy(
                 out=bias[:, br], in_=pb[:].rearrange("p (c m r) -> p r c m", c=2, m=16, r=16)
             )
-        sort_words(0)
-        transposes(0)
-        copy_out(0)
-        sort_words(1)
-        transposes(1)
-        copy_out(1)
-        for s in range(2):
-            for bcc in range(2):
-                w_piece(s, bcc)
-            w_quantise(s)
         quantise(0)
         quantise(1)
         sort_words(2)
@@ -218,6 +227,9 @@ def tile_switchnet_fstar_pa_t_kernel(tc, x, k1, b1, out):
 
         for i in range(NSUB):
             n = i // SUB
+            if i == 0:
+                for br in range(2):
+                    multiply(i, br)
             if i + LAG < NSUB:
                 transposes(i + LAG)
                 copy_out(i + LAG)
@@ -228,8 +240,9 @@ def tile_switchnet_fstar_pa_t_kernel(tc, x, k1, b1, out):
             if i % SUB == 0:
                 ob = outs.tile([P, SUB, 16, 2, 2, 16], F32)
                 obs[n] = ob
-            for br in range(2):
-                multiply(i, br)
+            if i > 0:
+                for br in range(2):
+                    multiply(i, br)
             for h in range(2) if i == NSUB - 1 else [None]:
                 for br in range(2):
                     add_bias(i, br, h)

from contextlib import ExitStack

import concourse.mybir as mybir
from concourse.masks import make_identity

FLOPS = 2 * 4096 * 4 * 512 * 256

F32 = mybir.dt.float32
BF16 = mybir.dt.bfloat16
U32 = mybir.dt.uint32
U8 = mybir.dt.uint8
FP8X4 = mybir.dt.float8_e4m3fn_x4
ADD = mybir.AluOpType.add

P = 128
SUB = 4
NCH = 4096 // (P * SUB)
NSUB = NCH * SUB
XBUFS = 5
LAG = 2


def tile_switchnet_fstar_pa_t_kernel(tc, x, k1, b1, out):
    nc = tc.nc
    x_v = x.rearrange("(n p t) g c -> n p t (g c)", p=P, t=SUB)
    out_v = out.rearrange("(n p t) a b -> n p t (a b)", p=P, t=SUB)

    with ExitStack() as ctx:
        const = ctx.enter_context(tc.tile_pool(name="const", bufs=1))
        xin = ctx.enter_context(tc.tile_pool(name="xin", bufs=XBUFS))
        xre = ctx.enter_context(tc.tile_pool(name="xre", bufs=5))
        grp = ctx.enter_context(tc.tile_pool(name="grp", bufs=4))
        cod = ctx.enter_context(tc.tile_pool(name="cod", bufs=LAG + 3))
        outs = ctx.enter_context(tc.tile_pool(name="outs", bufs=5))
        psx = ctx.enter_context(tc.psum_pool(name="psx", bufs=4))
        psa = ctx.enter_context(tc.psum_pool(name="psa", bufs=4))
        ctx.enter_context(tc.manual_schedule())

        x_tiles = {}
        sorted_words = {}
        banks = {}
        groups = {}
        codes = {}
        planes = {}
        accs = {}
        obs = {}

        def load(n):
            xs = xin.tile([P, SUB * 2048], BF16)
            if n == 0:
                for t0, t1 in ((0, 1), (1, 2), (2, SUB)):
                    nc.sync.dma_start(
                        out=xs[:, t0 * 2048 : t1 * 2048].rearrange("p (t e) -> p t e", e=2048),
                        in_=x_v[n][:, t0:t1, :],
                    )
            else:
                nc.sync.dma_start(out=xs[:].rearrange("p (t e) -> p t e", t=SUB), in_=x_v[n])
            x_tiles[n] = xs

        def sort_words(i):
            w0 = (i % SUB) * 1024 + 512
            xs = xre.tile([P, 512], F32)
            nc.scalar.copy(
                out=xs[:].rearrange("p (c r w) -> p c r w", c=2, r=16, w=16),
                in_=x_tiles[i // SUB][:]
                .bitcast(F32)[:, w0 : w0 + 512]
                .rearrange("p (r c w) -> p c r w", r=16, c=2, w=16),
            )
            sorted_words[i] = xs

        def transposes(i):
            xw = x_tiles[i // SUB][:].bitcast(F32)
            for br in range(2):
                ps = psx.tile([P, 4, P], F32, tag="xt")
                for u in range(4):
                    if br == 0:
                        c0 = (i % SUB) * 1024 + u * P
                        words = xw[:, c0 : c0 + P]
                    else:
                        words = sorted_words[i][:, u * P : (u + 1) * P]
                    nc.tensor.transpose(ps[:, u, :], words, ident[:])
                banks[(i, br)] = ps

        def copy_out(i):
            g = grp.tile([P, 2048], BF16, align_bytes=64)
            groups[i] = g
            gf = g[:].bitcast(F32).rearrange("p (r s b u) -> p r s b u", r=2, s=2, b=P, u=2)
            for br in range(2):
                nc.scalar.copy(
                    out=gf[:, br], in_=banks[(i, br)][:].rearrange("p (s u) b -> p s b u", u=2)
                )

        def quantise(i):
            cw = cod.tile([P, 512], U32, align_bytes=64)
            cp = cod.tile([P, 512], U8, align_bytes=64)
            codes[i] = cw
            planes[i] = cp
            nc.vector.quantize_mx(out=cw[:].bitcast(FP8X4), scales=cp[:], in_=groups[i][:])

        def multiply(i, br):
            acc = psa.tile([P, 512], F32, tag="acc")
            for s in range(2):
                c0 = (br * 2 + s) * P
                if br == 0:
                    w0, width, o0 = s * 512, 512, 0
                else:
                    w0, width, o0 = 1024 + s * 256, 256, s * 256
                nc.tensor.matmul_mx(
                    out=acc[:, o0 : o0 + width],
                    lhsT=codes[i][:, c0 : c0 + P].bitcast(FP8X4),
                    lhsT_scale=planes[i][:, c0 : c0 + P],
                    rhs=wc[:, w0 : w0 + width].bitcast(FP8X4),
                    rhs_scale=wp[:, w0 : w0 + width],
                    start=(br == 1 or s == 0),
                    stop=(br == 1 or s == 1),
                )
            accs[(i, br)] = acc

        def add_bias(i, br, half):
            r = slice(0, 16) if half is None else slice(8 * half, 8 * half + 8)
            nc.vector.tensor_tensor(
                out=obs[i // SUB][:, i % SUB, r, br],
                in0=accs[(i, br)][:].rearrange(
                    "p (r c m) -> p r c m" if br == 0 else "p (c r m) -> p r c m", c=2, m=16, r=16
                )[:, r],
                in1=bias[:, br, r],
                op=ADD,
            )

        ident = const.tile([P, P], F32)
        make_identity(nc, ident[:])
        brow = const.tile([P, 1024], BF16)
        nc.vector.memset(brow[:].bitcast(F32), 0.0)
        wraw = const.tile([P, 8, 512], BF16)
        for br in (1, 0):
            nc.sync.dma_start(
                out=wraw[:, 4 * br : 4 * br + 4, :],
                in_=k1[2 * br : 2 * br + 2].rearrange("j (u p h) l -> p (j u) (h l)", u=2, p=P, h=2),
            )
        nc.sync.dma_start(out=brow[0:1, :], in_=b1.rearrange("o j l -> o (j l)"))
        for n in range(XBUFS):
            load(n)

        place = const.tile([P, 2, 2, P], BF16)
        nc.vector.memset(place[:].rearrange("p g b c -> p (g b c)").bitcast(F32), 0.0)
        for g in range(2):
            for bc in range(2):
                nc.vector.tensor_copy(
                    out=place[:, g, bc].rearrange("p (r b w) -> p r b w", r=4, b=2)[:, :, bc, :],
                    in_=ident[:, g * 64 : (g + 1) * 64].rearrange("p (r w) -> p r w", r=4),
                )
        ones = const.tile([P, P], BF16)
        nc.vector.memset(ones[:], 1.0)
        warm = const.tile([P, 2], F32)
        nc.scalar.copy(out=warm[:], in_=ident[:, 0:2])
        bias = const.tile([P, 2, 16, 2, 16], F32)
        wg = const.tile([P, 3 * 2048], BF16, align_bytes=64)
        wc = const.tile([P, 3 * 512], U32, align_bytes=64)
        wp = const.tile([P, 3 * 512], U8, align_bytes=64)

        def w_piece(s, bc, half):
            if s == 0:
                xt = psx.tile([P, 4, P], F32, tag="xt")
                bank = xt[:]
            else:
                acc = psa.tile([P, 512], F32, tag="acc")
                bank = acc[:].rearrange("p (t c) -> p t c", t=4)
            cols = slice(half * P, (half + 1) * P)
            for g in range(2):
                nc.tensor.matmul(
                    bank[:, 2 * g : 2 * g + 2, :],
                    lhsT=place[:, g, bc, :],
                    rhs=wraw[:, 2 * bc + s, :].rearrange("p (h l) -> p h l", h=2)[:, :, cols],
                    start=True,
                    stop=True,
                )
            dst = wg[:, s * 2048 : (s + 1) * 2048].rearrange("p (r b m t) -> p r b m t", r=16, b=2, m=16)
            dst = dst[:, :, bc, 8 * half : 8 * half + 8, :]
            src = bank.rearrange("p t (m r) -> p r m t", r=16)
            if half == 0:
                nc.scalar.copy(out=dst, in_=src)
            else:
                nc.vector.tensor_copy(out=dst, in_=src)

        def w_dense(bc):
            o0 = 4096 + bc * 1024
            nc.vector.tensor_copy(
                out=wg[:, o0 : o0 + 1024].rearrange("p (r m t) -> p r m t", r=16, t=4),
                in_=wraw[:, 4 + 2 * bc : 6 + 2 * bc, :].rearrange(
                    "p u (h m r) -> p r m (u h)", h=2, r=16
                ),
            )

        def w_quantise(q):
            nc.vector.quantize_mx(
                out=wc[:, q * 512 : (q + 1) * 512].bitcast(FP8X4),
                scales=wp[:, q * 512 : (q + 1) * 512],
                in_=wg[:, q * 2048 : (q + 1) * 2048],
            )

        w_dense(0)
        w_dense(1)
        w_quantise(2)
        for s in range(2):
            for bc in range(2):
                for half in range(2):
                    w_piece(s, bc, half)
            w_quantise(s)
            sort_words(s)
            if s == 0:
                transposes(0)
        copy_out(0)
        transposes(1)
        copy_out(1)
        for br in range(2):
            pb = psa.tile([P, 512], F32, tag="acc")
            nc.tensor.matmul(
                pb[:], lhsT=ones[:], rhs=brow[:, br * 512 : (br + 1) * 512], start=True, stop=True
            )
            nc.scalar.copy(
                out=bias[:, br], in_=pb[:].rearrange("p (c m r) -> p r c m", c=2, m=16, r=16)
            )
        quantise(0)
        quantise(1)
        sort_words(2)
        sort_words(3)

        for i in range(NSUB):
            n = i // SUB
            if i == 0:
                for br in range(2):
                    multiply(i, br)
            if i + LAG < NSUB:
                transposes(i + LAG)
                copy_out(i + LAG)
                if i + LAG + 2 < NSUB:
                    sort_words(i + LAG + 2)
                if (i + LAG) % SUB == SUB - 1 and (i + LAG) // SUB + XBUFS < NCH:
                    load((i + LAG) // SUB + XBUFS)
            if i % SUB == 0:
                ob = outs.tile([P, SUB, 16, 2, 2, 16], F32)
                obs[n] = ob
            if i > 0:
                for br in range(2):
                    multiply(i, br)
            for h in range(2) if i == NSUB - 1 else [None]:
                for br in range(2):
                    add_bias(i, br, h)
                if h is not None:
                    nc.sync.dma_start(
                        out=out_v[n][:, i % SUB, h * 512 : (h + 1) * 512],
                        in_=obs[n][:, i % SUB, 8 * h : 8 * h + 8].rearrange("p r b c m -> p (r b c m)"),
                    )
            if i + LAG < NSUB:
                quantise(i + LAG)
            if i < NSUB - SUB:
                done = (0, SUB) if i % SUB == SUB - 1 else None
            else:
                done = {1: (0, 2), 2: (2, 3)}.get(i % SUB)
            if done is not None:
                t0, t1 = done
                nc.sync.dma_start(
                    out=out_v[n][:, t0:t1, :],
                    in_=obs[n][:, t0:t1].rearrange("p t r b c m -> p t (r b c m)"),
                )
